import numpy as np
import ml_dtypes


def mxq(x, axis, fmt="e4m3"):
    dtype, down = {"e4m3": (ml_dtypes.float8_e4m3fn, 7), "e5m2": (ml_dtypes.float8_e5m2, 14)}[fmt]
    v = np.moveaxis(np.asarray(x, np.float32).astype(ml_dtypes.bfloat16).astype(np.float64), axis, -1)
    blocks = v.reshape(v.shape[:-1] + (-1, 32))
    amax = np.abs(blocks).max(-1, keepdims=True)
    byte = np.maximum(np.where(amax > 0, np.frexp(amax)[1] - 1 + 127, 0) - down, 1)
    scale = np.exp2(byte - 127.0)
    codes = (blocks / scale).astype(np.float32).astype(dtype).astype(np.float64)
    return np.moveaxis((codes * scale).reshape(v.shape), -1, axis)


WIDE = False


def mx_kscale(k):
    if not WIDE:
        return np.ones(k)
    levels = np.array([30, -30])
    if k % 512:
        return np.exp2(np.random.permutation(np.resize(levels, k // 32))).repeat(32)
    a = np.empty((k // 512, 16))
    for p in range(k // 512):
        a[p, :8] = np.random.permutation(np.resize(levels, 8))
        for g in range(8):
            far = levels[np.abs(levels - a[p, g]) >= 10]
            a[p, g + 8] = far[np.random.randint(len(far))]
    return np.exp2(a.ravel()).repeat(32)


BF16 = ml_dtypes.bfloat16


def bf(x):
    return np.asarray(x, np.float32).astype(BF16)


def f64(x):
    return np.asarray(x).astype(np.float64)


B, V, H = 512, 128, 1024
G = 4 * H
EPS = 1e-5


def sigmoid(v):
    return 1.0 / (1.0 + np.exp(-v))


def layer_norm(v, w, b):
    mu = v.mean(-1, keepdims=True)
    var = ((v - mu) ** 2).mean(-1, keepdims=True)
    return (v - mu) / np.sqrt(var + EPS) * w + b


def setup_inputs():
    s = mx_kscale(H)
    return {"x": bf(np.random.standard_normal((B, V))),
            "h0": bf(np.random.standard_normal((B, H)) * s),
            "c0": bf(np.random.standard_normal((B, H))),
            "w_ih1": bf(np.random.standard_normal((G, V)) / np.sqrt(V)),
            "w_hh1": bf(np.random.standard_normal((G, H)) / np.sqrt(H) / s),
            "lni_w1": bf(1.0 + 0.1 * np.random.standard_normal(G)),
            "lni_b1": bf(0.1 * np.random.standard_normal(G)),
            "lnh_w1": bf(1.0 + 0.1 * np.random.standard_normal(G)),
            "lnh_b1": bf(0.1 * np.random.standard_normal(G)),
            "lnc_w1": bf(1.0 + 0.1 * np.random.standard_normal(H)),
            "lnc_b1": bf(0.1 * np.random.standard_normal(H))}


def reference(x, h0, c0, w_ih1, w_hh1, lni_w1, lni_b1, lnh_w1, lnh_b1, lnc_w1, lnc_b1):
    a = f64(x) @ f64(w_ih1).T
    r = mxq(f64(h0), 1, "e5m2") @ mxq(f64(w_hh1), 1, "e5m2").T
    gates = layer_norm(a, f64(lni_w1), f64(lni_b1)) + layer_norm(r, f64(lnh_w1), f64(lnh_b1))
    i, f, g, o = np.split(gates, 4, axis=1)
    cy = layer_norm(sigmoid(f) * f64(c0) + sigmoid(i) * np.tanh(g), f64(lnc_w1), f64(lnc_b1))
    hy = sigmoid(o) * np.tanh(cy)
    return hy, cy

@@ -1,0 +1,568 @@
+from contextlib import ExitStack
+
+import concourse.mybir as mybir
+from concourse.masks import make_identity
+
+B, V, H = 512, 128, 1024
+G = 4 * H
+EPS = 1e-5
+FLOPS = 2 * B * G * (H + V)
+
+F32 = mybir.dt.float32
+BF16 = mybir.dt.bfloat16
+U32 = mybir.dt.uint32
+U8 = mybir.dt.uint8
+FP8X4 = mybir.dt.float8_e5m2_x4
+ACT = mybir.ActivationFunctionType
+ALU = mybir.AluOpType
+AXIS = mybir.AxisListType
+
+P = 128
+TILES = B // P
+BANK = 512
+BLOCKS = G // BANK
+PASSES = H // 512
+GATE_I, GATE_F, GATE_G, GATE_O = 0, 1, 2, 3
+CHUNKS = G // P
+A_PER_STEP = (0, 2, 2, 2, 2, 2, 2, 2, 2, 1, 1, 1, 1, 1, 1, 1, 1, 0, 0)
+SCALAR_COPIES = (1, 1, 1, 1, 1, 0, 0, 1, 0, 1, 1, 1, 1, 1, 1, 1, 1, 1)
+RSTD_A_STEP = 8
+LATE_BANKS = (3, 4)
+SU_LATE = ("scalar", "scalar", "scalar", "vector")
+SCALE_U = "vector"
+STAGE_BUFS = 3
+
+
+def tile_multilstm_pa_kernel(tc, x, h0, c0, w_ih1, w_hh1, lni_w1, lni_b1, lnh_w1, lnh_b1, lnc_w1, lnc_b1, out_0, out_1):
+    nc = tc.nc
+    with ExitStack() as ctx:
+        keep = ctx.enter_context(tc.tile_pool(name="keep", bufs=1))
+        shared = ctx.enter_context(tc.tile_pool(name="shared", bufs=1))
+        psum = ctx.enter_context(tc.psum_pool(name="psum", bufs=1))
+        ctx.enter_context(tc.manual_schedule(engines={mybir.EngineType.SP}))
+
+        def bank(i, dtype=F32):
+            width = BANK if dtype == F32 else 2 * BANK
+            return psum.tile([P, width], dtype, name="bank%d" % i, tag="bank%d" % i)
+
+        def stage_tile():
+            return shared.tile([P, 4, H], BF16, name="stage", tag="stage", bufs=STAGE_BUFS, align_bytes=64, offset=0)
+
+        ident_f32 = keep.tile([P, P], F32, name="ident_f32")
+        ident_bf16 = keep.tile([P, P], BF16, name="ident_bf16")
+        wih_sums = keep.tile([P, 4], F32, name="wih_sums")
+        neg_half = keep.tile([P, 2], F32, name="neg_half")
+        vec_rows = keep.tile([P, P], BF16, name="vec_rows")
+        bias_i = keep.tile([P, G // P], F32, name="bias_i")
+        bias = keep.tile([P, G // P], F32, name="bias")
+        x_rows = keep.tile([P, TILES, V], BF16, name="x_rows")
+        x_t = keep.tile([P, B], BF16, name="x_t")
+        x_t32 = keep.tile([P, B], F32, name="x_t32")
+        wih_t = keep.tile([P, G], BF16, name="wih_t")
+        neg_wbar = keep.tile([P, 1], F32, name="neg_wbar")
+        neg_mu_a = keep.tile([P, TILES], F32, name="neg_mu_a")
+        gain_i = keep.tile([P, G], BF16, name="gain_i")
+        gain_h = keep.tile([P, G], BF16, name="gain_h")
+        gain_c = keep.tile([P, H], BF16, name="gain_c")
+        bias_c = keep.tile([P, H], BF16, name="bias_c")
+        c_rows = keep.tile([P, TILES, H], BF16, name="c_rows")
+        h_codes = keep.tile([P, PASSES, B], U32, name="h_codes", align_bytes=64)
+        h_scales = keep.tile([P, PASSES, B], U8, name="h_scales", align_bytes=64)
+        w_codes = keep.tile([P, BLOCKS, PASSES, BANK], U32, name="w_codes", align_bytes=64)
+        w_scales = keep.tile([P, BLOCKS, PASSES, BANK], U8, name="w_scales", align_bytes=64)
+        u = keep.tile([P, TILES, G], F32, name="u")
+        ssq_a = keep.tile([P, TILES, BLOCKS], F32, name="ssq_a")
+        sums_r = keep.tile([P, 2, TILES, BLOCKS], F32, name="sums_r")
+        neg_shift = keep.tile([P, TILES], F32, name="neg_shift")
+        neg_mu_r = keep.tile([P, TILES], F32, name="neg_mu_r")
+        r_pairs = [keep.tile([P, 2, G], F32, name="r_first"), None]
+
+        for k, vec in enumerate((lni_w1, lni_b1, lnh_b1)):
+            nc.scalar.dma_start(out=vec_rows[k * CHUNKS:(k + 1) * CHUNKS, :], in_=vec.rearrange("(c p) -> c p", p=P))
+        nc.sync.dma_start(out=x_rows[:], in_=x.rearrange("(p t) v -> p t v", t=TILES))
+        wih_stage = stage_tile()
+        wih_rows = wih_stage[:].rearrange("p b (j c v) -> p (b j) c v", c=4, v=V)
+        for k in range(4):
+            nc.sync.dma_start(out=wih_rows[:, 2 * k:2 * (k + 1), :, :],
+                              in_=w_ih1[2 * k * BANK:2 * (k + 1) * BANK, :].rearrange("(j p c) v -> p j c v", p=P, c=4))
+        h_stage = stage_tile()
+        nc.sync.dma_start(out=h_stage[:], in_=h0.rearrange("(p t) k -> p t k", t=TILES))
+        w_stage = [None] * BLOCKS
+
+        def load_w(c):
+            w_stage[c] = stage_tile()
+            nc.sync.dma_start(out=w_stage[c][:], in_=w_hh1[c * BANK:(c + 1) * BANK, :].rearrange("(b p) k -> p b k", p=P))
+
+        load_w(0)
+        make_identity(nc, ident_bf16[:])
+        nc.gpsimd.memset(vec_rows[3 * CHUNKS:, :], 0.0)
+        make_identity(nc, ident_f32[:])
+        nc.gpsimd.memset(neg_half[:], -0.5)
+
+        def transpose_words(stage, q, banks):
+            tiles = []
+            for hb in range(2):
+                bk = bank(banks[hb])
+                view = bk[:].rearrange("p (b w r) -> p b w r", b=2, w=2)
+                for b in range(2):
+                    words = stage[:, 2 * hb + b, :].bitcast(F32)
+                    for w in range(2):
+                        nc.tensor.transpose(view[:, b, w, :], words[:, 256 * q + w:256 * (q + 1):2], ident_f32[:])
+                tiles.append(bk)
+            return tiles
+
+        def new_grouped():
+            return shared.tile([P, 4 * BANK], BF16, name="grouped", tag="grouped", bufs=3, align_bytes=64,
+                               offset=STAGE_BUFS * 4 * H * 2)
+
+        def interleave(engine, grouped, hb, bk):
+            dst = grouped[:].bitcast(F32)[:, hb * BANK:(hb + 1) * BANK].rearrange("p (b r w) -> p b r w", b=2, w=2)
+            src = bk[:].rearrange("p (b w r) -> p b r w", b=2, w=2)
+            if engine == "vector":
+                nc.vector.tensor_copy(out=dst, in_=src)
+            else:
+                nc.scalar.copy(out=dst, in_=src)
+
+        def quantize(grouped, codes, scales):
+            nc.vector.quantize_mx(out=codes.bitcast(FP8X4), scales=scales, in_=grouped[:])
+
+        def discard():
+            return keep.tile([P, BANK], BF16, name="discard", tag="discard", bufs=3)
+
+        def a_matmul(t, j, i):
+            bk = bank(i)
+            nc.tensor.matmul(bk[:], lhsT=x_t[:, t * P:(t + 1) * P], rhs=wih_t[:, j * BANK:(j + 1) * BANK], start=True, stop=True)
+            return bk
+
+        def a_square(t, j, bk):
+            sq = discard()
+            nc.scalar.activation(out=sq[:], in_=bk[:], func=ACT.Square, bias=neg_mu_a[:, t:t + 1], accum_out=ssq_a[:, t, j:j + 1])
+
+        def a_gain(t, j, bk):
+            cols = slice(j * BANK, (j + 1) * BANK)
+            nc.vector.scalar_tensor_tensor(out=u[:, t, cols], in0=bk[:], scalar=neg_mu_a[:, t:t + 1], in1=gain_i[:, cols],
+                                           op0=ALU.add, op1=ALU.mult)
+
+        def r_matmul(t, j, i):
+            bk = bank(i)
+            rows = slice(t * P, (t + 1) * P)
+            for q in range(PASSES):
+                nc.tensor.matmul_mx(out=bk[:], lhsT=h_codes[:, q, rows].bitcast(FP8X4), lhsT_scale=h_scales[:, q, rows],
+                                    rhs=w_codes[:, j, q, :].bitcast(FP8X4), rhs_scale=w_scales[:, j, q, :],
+                                    start=(q == 0), stop=(q == PASSES - 1))
+            return bk
+
+        def r_cols(t, cols):
+            return r_pairs[t // 2][:, t % 2, cols]
+
+        def r_copy(t, j, bk):
+            nc.scalar.activation(out=r_cols(t, slice(j * BANK, (j + 1) * BANK)), in_=bk[:], func=ACT.Copy,
+                                 accum_out=sums_r[:, 0, t, j:j + 1])
+
+        def r_shift(t):
+            nc.scalar.activation(out=neg_shift[:, t:t + 1], in_=sums_r[:, 0, t, 0:1], func=ACT.Copy, scale=-1.0 / BANK)
+
+        def r_square(t, j):
+            sq = discard()
+            nc.scalar.activation(out=sq[:], in_=r_cols(t, slice(j * BANK, (j + 1) * BANK)), func=ACT.Square,
+                                 bias=neg_shift[:, t:t + 1], accum_out=sums_r[:, 1, t, j:j + 1])
+
+        def small(name, width):
+            return keep.tile([P, width], F32, name=name, tag=name, bufs=3)
+
+        def rstd_a(pair):
+            total = small("a_total", 2)
+            nc.vector.tensor_reduce(out=total[:], in_=ssq_a[:, 2 * pair:2 * pair + 2, :], axis=AXIS.X, op=ALU.add)
+            var = small("a_var", 2)
+            nc.vector.tensor_scalar(out=var[:], in0=total[:], scalar1=1.0 / G, scalar2=EPS, op0=ALU.mult, op1=ALU.add)
+            rstd = small("a_rstd", 2)
+            nc.gpsimd.tensor_tensor(out=rstd[:], in0=var[:], in1=neg_half[:], op=ALU.pow)
+            return rstd
+
+        def scale_u(t, cols, rstd, engine=SCALE_U):
+            if engine == "scalar":
+                nc.scalar.activation(out=u[:, t, cols], in_=u[:, t, cols], func=ACT.Copy, scale=rstd[:, t % 2:t % 2 + 1])
+            elif engine == "vector":
+                nc.vector.tensor_scalar(out=u[:, t, cols], in0=u[:, t, cols], scalar1=rstd[:, t % 2:t % 2 + 1], scalar2=None, op0=ALU.mult)
+            else:
+                nc.gpsimd.tensor_scalar(out=u[:, t, cols], in0=u[:, t, cols], scalar1=rstd[:, t % 2:t % 2 + 1], scalar2=0.0,
+                                        op0=ALU.mult, op1=ALU.add)
+
+        x_bank = bank(0, BF16)
+        for t in range(TILES):
+            nc.tensor.transpose(x_bank[:, t * P:(t + 1) * P], x_rows[:, t, :], ident_bf16[:])
+        nc.vector.tensor_copy(out=x_t[:], in_=x_bank[:, :B])
+        nc.vector.tensor_copy(out=x_t32[:], in_=x_bank[:, :B])
+
+        def gain_bank(k, i):
+            bk = bank(i, BF16)
+            for c in range(8):
+                nc.tensor.matmul(bk[:, c * P:(c + 1) * P], lhsT=ident_bf16[:, 8 * k + c:8 * k + c + 1].to_broadcast([P, P]),
+                                 rhs=vec_rows[:], start=True, stop=True)
+            return bk
+
+        def wih_bank(k, i):
+            bk = bank(i, BF16)
+            for jc in range(8):
+                nc.tensor.transpose(bk[:, jc * P:(jc + 1) * P], wih_rows[:, 2 * k + jc // 4, jc % 4, :], ident_bf16[:])
+            dst = wih_t[:, 2 * k * BANK:2 * (k + 1) * BANK].rearrange("p (j r c) -> p j r c", j=2, c=4)
+            src = bk[:].rearrange("p (j c r) -> p j r c", j=2, c=4)
+            if k % 2 == 0:
+                nc.scalar.activation(out=dst, in_=src, func=ACT.Copy, accum_out=wih_sums[:, k:k + 1])
+            else:
+                nc.vector.tensor_scalar(out=dst, in0=src, scalar1=1.0, scalar2=None, op0=ALU.mult, op1=ALU.add, accum_out=wih_sums[:, k:k + 1])
+
+        def gain_part(k, i):
+            bk = gain_bank(k, i)
+            cols = slice(2 * k * BANK, 2 * (k + 1) * BANK)
+            if k % 2 == 1:
+                nc.scalar.copy(out=gain_i[:, cols], in_=bk[:])
+            else:
+                nc.vector.tensor_copy(out=gain_i[:, cols], in_=bk[:])
+
+        for k in range(4):
+            wih_bank(k, 1 + k)
+            gain_part(k, (5, 6, 7, 0)[k])
+        scaled_sums = small("scaled_sums", 4)
+        nc.vector.tensor_scalar(out=scaled_sums[:], in0=wih_sums[:], scalar1=-1.0 / G, scalar2=None, op0=ALU.mult, op1=ALU.add,
+                                accum_out=neg_wbar[:])
+        load_w(1)
+
+        steps = PASSES + BLOCKS * PASSES
+        a_units = [(t, j) for t in range(TILES) for j in range(BLOCKS)]
+        groupeds = {}
+        rstds_a = {}
+        next_bank = [0]
+
+        def rolling():
+            next_bank[0] += 1
+            return 4 + next_bank[0] % 4
+
+        for s in range(steps + 1):
+            c, q = divmod(s - PASSES, PASSES)
+            units = []
+            for k in range(A_PER_STEP[s]):
+                t, j = a_units.pop(0)
+                units.append((t, j, a_matmul(t, j, rolling())))
+            r_unit = None
+            if PASSES + 3 <= s:
+                j, t = divmod(s - PASSES - 3, 2)
+                r_unit = (t, j, r_matmul(t, j, rolling()))
+            t_tiles = None
+            if s < steps:
+                t_tiles = transpose_words(h_stage if c < 0 else w_stage[c], q, (2 * q, 2 * q + 1))
+                groupeds[s] = new_grouped()
+                if q == PASSES - 1 and c + STAGE_BUFS < BLOCKS:
+                    load_w(c + STAGE_BUFS)
+                if q == PASSES - 1 and c + STAGE_BUFS == BLOCKS:
+                    nc.sync.dma_start(out=gain_h[:], in_=lnh_w1.partition_broadcast(P))
+                    nc.sync.dma_start(out=c_rows[:], in_=c0.rearrange("(p t) h -> p t h", t=TILES))
+                    nc.sync.dma_start(out=gain_c[:], in_=lnc_w1.partition_broadcast(P))
+                    nc.sync.dma_start(out=bias_c[:], in_=lnc_b1.partition_broadcast(P))
+            if len(units) == 2:
+                a_square(*units[0])
+                a_gain(*units[1])
+                a_gain(*units[0])
+                a_square(*units[1])
+            if len(units) == 1:
+                a_gain(*units[0])
+            if r_unit is not None:
+                r_copy(*r_unit)
+            if len(units) == 1:
+                a_square(*units[0])
+            if 1 <= s <= steps:
+                cq, qq = divmod(s - 1 - PASSES, PASSES)
+                if cq < 0:
+                    quantize(groupeds[s - 1], h_codes[:, qq, :], h_scales[:, qq, :])
+                else:
+                    quantize(groupeds[s - 1], w_codes[:, cq, qq, :], w_scales[:, cq, qq, :])
+            if PASSES + 4 <= s:
+                j, t = divmod(s - PASSES - 4, 2)
+                r_square(t, j)
+            if r_unit is not None and r_unit[1] == 0:
+                r_shift(r_unit[0])
+            if t_tiles is not None:
+                on_scalar = SCALAR_COPIES[s]
+                interleave("scalar" if on_scalar == 2 else "vector", groupeds[s], 0, t_tiles[0])
+                interleave("scalar" if on_scalar >= 1 else "vector", groupeds[s], 1, t_tiles[1])
+            if s == 0:
+                mu_bank = bank(rolling())
+                for t in range(TILES):
+                    nc.tensor.matmul(mu_bank[:, t:t + 1], lhsT=x_t32[:, t * P:(t + 1) * P], rhs=neg_wbar[:], start=True, stop=True)
+                nc.vector.tensor_copy(out=neg_mu_a[:], in_=mu_bank[:, :TILES])
+            if s == 4:
+                bias_bank = bank(rolling(), BF16)
+                nc.tensor.transpose(bias_bank[:, :P], vec_rows[:], ident_bf16[:])
+                nc.scalar.copy(out=bias_i[:], in_=bias_bank[:, CHUNKS:2 * CHUNKS])
+                nc.vector.tensor_tensor(out=bias[:], in0=bias_bank[:, 2 * CHUNKS:3 * CHUNKS], in1=bias_i[:], op=ALU.add)
+            if s == RSTD_A_STEP:
+                rstds_a[0] = rstd_a(0)
+            if RSTD_A_STEP < s <= RSTD_A_STEP + 8:
+                k = s - RSTD_A_STEP - 1
+                scale_u(k % 2, slice((k // 2) * H, (k // 2 + 1) * H), rstds_a[0])
+
+        r_pairs[1] = shared.tile([P, 2, G], F32, name="r_second", tag="r_second", align_bytes=64, offset=0)
+
+        def stats_r(group, fill_1, fill_2):
+            n = len(group)
+            tiles = slice(group[0], group[0] + n)
+            total = small("r_total", 4)
+            nc.vector.tensor_reduce(out=total[:, :2 * n].rearrange("p (k t) -> p k t", k=2), in_=sums_r[:, :, tiles, :], axis=AXIS.X, op=ALU.add)
+            fill_1()
+            nc.vector.tensor_scalar(out=neg_mu_r[:, tiles], in0=total[:, :n], scalar1=-1.0 / G, scalar2=None, op0=ALU.mult)
+            parts = small("r_parts", 6)
+            nc.vector.scalar_tensor_tensor(out=parts[:, 0:n], in0=total[:, :n], scalar=1.0 / G, in1=neg_shift[:, tiles], op0=ALU.mult, op1=ALU.add)
+            nc.vector.scalar_tensor_tensor(out=parts[:, 2:2 + n], in0=total[:, :n], scalar=-1.0 / G, in1=neg_shift[:, tiles], op0=ALU.mult, op1=ALU.subtract)
+            nc.vector.tensor_scalar(out=parts[:, 4:4 + n], in0=total[:, n:2 * n], scalar1=1.0 / G, scalar2=EPS, op0=ALU.mult, op1=ALU.add)
+            fill_2()
+            var = small("r_var", 2)
+            for k in range(n):
+                nc.vector.scalar_tensor_tensor(out=var[:, k:k + 1], in0=parts[:, k:k + 1], scalar=parts[:, 2 + k:3 + k], in1=parts[:, 4 + k:5 + k],
+                                               op0=ALU.mult, op1=ALU.add)
+            rstd = small("r_rstd", 2)
+            nc.gpsimd.tensor_tensor(out=rstd[:, :n], in0=var[:, :n], in1=neg_half[:, :n], op=ALU.pow)
+            for k, t in enumerate(group):
+                rstd_r[t] = rstd[:, k:k + 1]
+
+        rstd_r = {}
+
+        def gate_cols(gate):
+            return slice(gate * H, (gate + 1) * H)
+
+        def r_gain(t, gate):
+            ap = r_cols(t, gate_cols(gate))
+            nc.vector.scalar_tensor_tensor(out=ap, in0=ap, scalar=neg_mu_r[:, t:t + 1], in1=gain_h[:, gate_cols(gate)],
+                                           op0=ALU.add, op1=ALU.mult)
+
+        def r_scale(t, gate, engine="vector"):
+            ap = r_cols(t, gate_cols(gate))
+            if engine == "gpsimd":
+                nc.gpsimd.tensor_scalar(out=ap, in0=ap, scalar1=rstd_r[t], scalar2=0.0, op0=ALU.mult, op1=ALU.add)
+            elif engine == "vector":
+                nc.vector.tensor_scalar(out=ap, in0=ap, scalar1=rstd_r[t], scalar2=None, op0=ALU.mult)
+            else:
+                nc.scalar.activation(out=ap, in_=ap, func=ACT.Copy, scale=rstd_r[t])
+
+        def gate_sum(pair, gate, k, i):
+            bk = bank(i)
+            view = bk[:].rearrange("p (c t b) -> p c t b", c=2, t=2)
+            for cc in range(2):
+                chunk = gate * 8 + 2 * k + cc
+                cols = slice(chunk * P, (chunk + 1) * P)
+                for tt in range(2):
+                    t = 2 * pair + tt
+                    nc.tensor.matmul(view[:, cc, tt, :], lhsT=u[:, t, cols], rhs=ident_f32[:], start=True, stop=False, is_transpose=True)
+                    nc.tensor.matmul(view[:, cc, tt, :], lhsT=r_cols(t, cols), rhs=ident_f32[:], start=False, stop=True, is_transpose=True)
+            for cc in range(2):
+                chunk = gate * 8 + 2 * k + cc
+                nc.scalar.activation(out=r_pairs[pair][:, :, chunk * P:(chunk + 1) * P], in_=view[:, cc, :, :],
+                                     func=ACT.Tanh if gate == GATE_G else ACT.Sigmoid, bias=bias[:, chunk:chunk + 1])
+
+        gate_count = [0]
+
+        def gate_half(pair, gate, half, banks=(0, 1, 2)):
+            for k in (2 * half, 2 * half + 1):
+                gate_count[0] += 1
+                gate_sum(pair, gate, k, banks[gate_count[0] % len(banks)])
+
+        def mean_passes(t, bk, blocks):
+            rows = slice(t * P, (t + 1) * P)
+            for j in blocks:
+                for q in range(PASSES):
+                    nc.tensor.matmul_mx(out=bk[:], lhsT=h_codes[:, q, rows].bitcast(FP8X4), lhsT_scale=h_scales[:, q, rows],
+                                        rhs=w_codes[:, j, q, :].bitcast(FP8X4), rhs_scale=w_scales[:, j, q, :],
+                                        start=(j == 0 and q == 0), stop=(j == BLOCKS - 1 and q == PASSES - 1))
+
+        def mean_read(t, bk):
+            sq = discard()
+            nc.scalar.activation(out=sq[:], in_=bk[:], func=ACT.Copy, scale=-1.0 / G, accum_out=neg_mu_r[:, t:t + 1])
+
+        late_tiles = {}
+
+        def late_matmul(t, j):
+            late_tiles[(t, j)] = r_matmul(t, j, LATE_BANKS[j % len(LATE_BANKS)])
+
+        def late_square(t, j):
+            sq = discard()
+            nc.scalar.activation(out=sq[:], in_=late_tiles[(t, j)][:], func=ACT.Square, bias=neg_mu_r[:, t:t + 1],
+                                 accum_out=sums_r[:, 1, t, j:j + 1])
+
+        def late_gain(t, j):
+            cols = slice(j * BANK, (j + 1) * BANK)
+            nc.vector.scalar_tensor_tensor(out=r_cols(t, cols), in0=late_tiles[(t, j)][:], scalar=neg_mu_r[:, t:t + 1], in1=gain_h[:, cols],
+                                           op0=ALU.add, op1=ALU.mult)
+
+        def late(t, j):
+            late_matmul(t, j)
+            late_square(t, j)
+            late_gain(t, j)
+
+        def sum_blocks(parts):
+            total = small("total", 2)
+            nc.vector.tensor_reduce(out=total[:], in_=parts, axis=AXIS.X, op=ALU.add)
+            return total
+
+        def rstd_from(total):
+            var = small("var", 2)
+            nc.vector.tensor_scalar(out=var[:], in0=total[:], scalar1=1.0 / G, scalar2=EPS, op0=ALU.mult, op1=ALU.add)
+            rstd = small("rstd", 2)
+            nc.gpsimd.tensor_tensor(out=rstd[:], in0=var[:], in1=neg_half[:], op=ALU.pow)
+            return rstd
+
+        def input_times_cell(t):
+            ap = r_cols(t, gate_cols(GATE_I))
+            nc.vector.tensor_tensor(out=ap, in0=ap, in1=r_cols(t, gate_cols(GATE_G)), op=ALU.mult)
+
+        def c0_transposed(t, i):
+            bk = bank(i, BF16)
+            for j in range(H // P):
+                nc.tensor.transpose(bk[:, j * P:(j + 1) * P], c_rows[:, t, j * P:(j + 1) * P], ident_bf16[:])
+            return bk
+
+        def forget_times_c0(t, bk):
+            ap = r_cols(t, gate_cols(GATE_F))
+            nc.vector.tensor_tensor(out=ap, in0=bk[:], in1=ap, op=ALU.mult)
+
+        def back(t, gates, banks):
+            tiles = []
+            for half in range(2):
+                bk = bank(banks[half])
+                for jj in range(4):
+                    j = 4 * half + jj
+                    for k, gate in enumerate(gates):
+                        nc.tensor.matmul(bk[:, jj * P:(jj + 1) * P], lhsT=r_cols(t, slice(gate * H + j * P, gate * H + (j + 1) * P)),
+                                         rhs=ident_f32[:], start=(k == 0), stop=(k == len(gates) - 1), is_transpose=True)
+                tiles.append(bk)
+            return tiles
+
+        def cell_parts(tiles):
+            parts = small("c_parts", 12)
+            for half in range(2):
+                nc.vector.bn_stats(out=parts[:, 6 * half:6 * half + 6], in_=tiles[half][:])
+            return parts
+
+        def cell_mean_var(parts):
+            mean_var = small("c_mean_var", 2)
+            nc.vector.bn_aggr(out=mean_var[:], in_=parts[:])
+            return mean_var
+
+        def cell_rstd(mean_var):
+            var = small("c_var", 1)
+            nc.vector.tensor_scalar(out=var[:], in0=mean_var[:, 1:2], scalar1=EPS, scalar2=None, op0=ALU.add)
+            rstd = small("c_rstd", 1)
+            nc.gpsimd.tensor_tensor(out=rstd[:], in0=var[:], in1=neg_half[:, 0:1], op=ALU.pow)
+            return mean_var, rstd
+
+        def cell_centre(t, tiles, stats):
+            for half in range(2):
+                cols = slice(half * BANK, (half + 1) * BANK)
+                nc.vector.scalar_tensor_tensor(out=u[:, t, cols], in0=tiles[half][:], scalar=stats[0][:, 0:1], in1=gain_c[:, cols],
+                                               op0=ALU.subtract, op1=ALU.mult)
+
+        def cell_finish(t, stats):
+            cy = u[:, t, 0:H]
+            nc.vector.scalar_tensor_tensor(out=cy, in0=cy, scalar=stats[1][:, 0:1], in1=bias_c[:], op0=ALU.mult, op1=ALU.add)
+            nc.sync.dma_start(out=out_1.rearrange("(p t) h -> p t h", t=TILES)[:, t, :], in_=cy)
+
+        def cell_tanh(t):
+            nc.scalar.activation(out=u[:, t, H:2 * H], in_=u[:, t, 0:H], func=ACT.Tanh)
+
+        def hidden(t, tiles):
+            for half in range(2):
+                ap = u[:, t, H + half * BANK:H + (half + 1) * BANK]
+                nc.vector.tensor_tensor(out=ap, in0=tiles[half][:], in1=ap, op=ALU.mult)
+            nc.sync.dma_start(out=out_0.rearrange("(p t) h -> p t h", t=TILES)[:, t, :], in_=u[:, t, H:2 * H])
+
+        def prepare(group, gate, engine="vector"):
+            for t in group:
+                r_gain(t, gate)
+            for t in group:
+                r_scale(t, gate, engine)
+
+        def nothing():
+            return None
+
+        last = BLOCKS - 1
+        r_last = [r_matmul(t, last, 4 + t) for t in range(2)]
+        r_copy(0, last, r_last[0])
+        r_square(1, last - 1)
+        r_copy(1, last, r_last[1])
+        r_square(0, last)
+        r_square(1, last)
+        stats_r((0, 1), nothing, nothing)
+        mean_bank = bank(4)
+        mean_passes(2, mean_bank, range(BLOCKS))
+        mean_read(2, mean_bank)
+        for k, (t, j) in enumerate(a_units):
+            bk = a_matmul(t, j, (0, 1, 2, 3, 6, 7)[k % 6])
+            a_gain(t, j, bk)
+            a_square(t, j, bk)
+        rstds_a[1] = rstd_from(sum_blocks(ssq_a[:, 2:4, :]))
+        order = (GATE_I, GATE_G, GATE_F, GATE_O)
+        mean_bank = bank(5)
+        for n in range(4):
+            prepare((0, 1), order[n], ("vector", "vector", "vector", "vector")[n])
+            late(2, 2 * n)
+            gate_half(0, order[n], 0)
+            late(2, 2 * n + 1)
+            gate_half(0, order[n], 1)
+            if n < 2:
+                mean_passes(3, mean_bank, range(4 * n, 4 * n + 4))
+            if n == 1:
+                mean_read(3, mean_bank)
+            if n >= 2:
+                late(3, 2 * n - 4)
+                late(3, 2 * n - 3)
+            if n == 2:
+                c0_banks = [c0_transposed(t, 6 + t) for t in (0, 1)]
+        for j in range(4, 8):
+            late(3, j)
+        rstd = rstd_from(sum_blocks(sums_r[:, 1, 2:4, :]))
+        for t in (2, 3):
+            rstd_r[t] = rstd[:, t - 2:t - 1]
+        for t in (0, 1):
+            input_times_cell(t)
+            forget_times_c0(t, c0_banks[t])
+        cell0 = back(0, (GATE_I, GATE_F), (5, 6))
+        cell1 = back(1, (GATE_I, GATE_F), (7, 3))
+        stats0 = cell_rstd(cell_mean_var(cell_parts(cell0)))
+        stats1 = cell_rstd(cell_mean_var(cell_parts(cell1)))
+        for n in range(3):
+            for t in (2, 3):
+                scale_u(t, gate_cols(order[n]), rstds_a[1], ("vector", "vector", "vector", "vector")[n])
+                r_scale(t, order[n], ("vector", "vector", "vector", "vector")[n])
+            gate_half(1, order[n], 0)
+            gate_half(1, order[n], 1)
+        cell_centre(0, cell0, stats0)
+        cell_finish(0, stats0)
+        cell_centre(1, cell1, stats1)
+        cell_finish(1, stats1)
+        c0_banks = [c0_transposed(t, 2 + t) for t in (2, 3)]
+        for t in (2, 3):
+            input_times_cell(t)
+            forget_times_c0(t, c0_banks[t - 2])
+        cell2 = back(2, (GATE_I, GATE_F), (6, 7))
+        cell3 = back(3, (GATE_I, GATE_F), (3, 4))
+        stats2 = cell_rstd(cell_mean_var(cell_parts(cell2)))
+        stats3 = cell_rstd(cell_mean_var(cell_parts(cell3)))
+        cell_tanh(0)
+        cell_tanh(1)
+        for t in (2, 3):
+            scale_u(t, gate_cols(GATE_O), rstds_a[1], ("vector", "vector", "vector", "vector")[3])
+            r_scale(t, GATE_O, ("vector", "vector", "vector", "vector")[3])
+        o0 = back(0, (GATE_O,), (5, 0))
+        hidden(0, o0)
+        o1 = back(1, (GATE_O,), (5, 0))
+        hidden(1, o1)
+        gate_half(1, GATE_O, 0, (1, 2))
+        gate_half(1, GATE_O, 1, (1, 2))
+        cell_centre(2, cell2, stats2)
+        cell_finish(2, stats2)
+        cell_tanh(2)
+        cell_centre(3, cell3, stats3)
+        cell_finish(3, stats3)
+        cell_tanh(3)
+        o2 = back(2, (GATE_O,), (5, 0))
+        o3 = back(3, (GATE_O,), (1, 2))
+        hidden(2, o2)
+        hidden(3, o3)

@@ -16,21 +16,20 @@ FP8X4 = mybir.dt.float8_e5m2_x4
 ACT = mybir.ActivationFunctionType
 ALU = mybir.AluOpType
 AXIS = mybir.AxisListType
+ENGINE = mybir.EngineType
 
 P = 128
 TILES = B // P
 BANK = 512
 BLOCKS = G // BANK
+CHUNKS = G // P
 PASSES = H // 512
 GATE_I, GATE_F, GATE_G, GATE_O = 0, 1, 2, 3
-CHUNKS = G // P
-A_PER_STEP = (0, 2, 2, 2, 2, 2, 2, 2, 2, 1, 1, 1, 1, 1, 1, 1, 1, 0, 0)
-SCALAR_COPIES = (1, 1, 1, 1, 1, 0, 0, 1, 0, 1, 1, 1, 1, 1, 1, 1, 1, 1)
-RSTD_A_STEP = 8
-LATE_BANKS = (3, 4)
-SU_LATE = ("scalar", "scalar", "scalar", "vector")
-SCALE_U = "vector"
 STAGE_BUFS = 3
+GROUPED_BUFS = 3
+STEPS = PASSES + BLOCKS * PASSES
+SCALAR_COPIES = (1, 1, 1, 1, 1, 0, 0, 1, 0, 1, 0, 1, 1, 0, 1, 1, 1, 1)
+FIRST_RSTD_STEP = 8
 
 
 def tile_multilstm_pa_kernel(tc, x, h0, c0, w_ih1, w_hh1, lni_w1, lni_b1, lnh_w1, lnh_b1, lnc_w1, lnc_b1, out_0, out_1):
@@ -39,7 +38,6 @@ def tile_multilstm_pa_kernel(tc, x, h0, c0, w_ih1, w_hh1, lni_w1, lni_b1, lnh_w1
         keep = ctx.enter_context(tc.tile_pool(name="keep", bufs=1))
         shared = ctx.enter_context(tc.tile_pool(name="shared", bufs=1))
         psum = ctx.enter_context(tc.psum_pool(name="psum", bufs=1))
-        ctx.enter_context(tc.manual_schedule(engines={mybir.EngineType.SP}))
 
         def bank(i, dtype=F32):
             width = BANK if dtype == F32 else 2 * BANK
@@ -48,17 +46,27 @@ def tile_multilstm_pa_kernel(tc, x, h0, c0, w_ih1, w_hh1, lni_w1, lni_b1, lnh_w1
         def stage_tile():
             return shared.tile([P, 4, H], BF16, name="stage", tag="stage", bufs=STAGE_BUFS, align_bytes=64, offset=0)
 
+        def grouped_tile():
+            return shared.tile([P, 4 * BANK], BF16, name="grouped", tag="grouped", bufs=GROUPED_BUFS, align_bytes=64,
+                               offset=STAGE_BUFS * 4 * H * 2)
+
+        def small(name, width):
+            return keep.tile([P, width], F32, name=name, tag=name, bufs=3)
+
+        def discard():
+            return keep.tile([P, BANK], BF16, name="discard", tag="discard", bufs=3)
+
         ident_f32 = keep.tile([P, P], F32, name="ident_f32")
         ident_bf16 = keep.tile([P, P], BF16, name="ident_bf16")
-        wih_sums = keep.tile([P, 4], F32, name="wih_sums")
         neg_half = keep.tile([P, 2], F32, name="neg_half")
         vec_rows = keep.tile([P, P], BF16, name="vec_rows")
-        bias_i = keep.tile([P, G // P], F32, name="bias_i")
-        bias = keep.tile([P, G // P], F32, name="bias")
+        bias_i = keep.tile([P, CHUNKS], F32, name="bias_i")
+        bias = keep.tile([P, CHUNKS], F32, name="bias")
         x_rows = keep.tile([P, TILES, V], BF16, name="x_rows")
         x_t = keep.tile([P, B], BF16, name="x_t")
         x_t32 = keep.tile([P, B], F32, name="x_t32")
         wih_t = keep.tile([P, G], BF16, name="wih_t")
+        wih_sums = keep.tile([P, 4], F32, name="wih_sums")
         neg_wbar = keep.tile([P, 1], F32, name="neg_wbar")
         neg_mu_a = keep.tile([P, TILES], F32, name="neg_mu_a")
         gain_i = keep.tile([P, G], BF16, name="gain_i")
@@ -72,76 +80,25 @@ def tile_multilstm_pa_kernel(tc, x, h0, c0, w_ih1, w_hh1, lni_w1, lni_b1, lnh_w1
         w_scales = keep.tile([P, BLOCKS, PASSES, BANK], U8, name="w_scales", align_bytes=64)
         u = keep.tile([P, TILES, G], F32, name="u")
         ssq_a = keep.tile([P, TILES, BLOCKS], F32, name="ssq_a")
-        sums_r = keep.tile([P, 2, TILES, BLOCKS], F32, name="sums_r")
-        neg_shift = keep.tile([P, TILES], F32, name="neg_shift")
-        neg_mu_r = keep.tile([P, TILES], F32, name="neg_mu_r")
-        r_pairs = [keep.tile([P, 2, G], F32, name="r_first"), None]
+        sums_r = keep.tile([P, 2, 2, BLOCKS], F32, name="sums_r")
+        neg_shift = keep.tile([P, 2], F32, name="neg_shift")
+        bn_r = keep.tile([P, 2, BLOCKS, 6], F32, name="bn_r")
+        r_pair = [keep.tile([P, 2, G], F32, name="r_first")]
+        rstd_a = []
 
-        for k, vec in enumerate((lni_w1, lni_b1, lnh_b1)):
-            nc.scalar.dma_start(out=vec_rows[k * CHUNKS:(k + 1) * CHUNKS, :], in_=vec.rearrange("(c p) -> c p", p=P))
-        nc.sync.dma_start(out=x_rows[:], in_=x.rearrange("(p t) v -> p t v", t=TILES))
-        wih_stage = stage_tile()
-        wih_rows = wih_stage[:].rearrange("p b (j c v) -> p (b j) c v", c=4, v=V)
-        for k in range(4):
-            nc.sync.dma_start(out=wih_rows[:, 2 * k:2 * (k + 1), :, :],
-                              in_=w_ih1[2 * k * BANK:2 * (k + 1) * BANK, :].rearrange("(j p c) v -> p j c v", p=P, c=4))
-        h_stage = stage_tile()
-        nc.sync.dma_start(out=h_stage[:], in_=h0.rearrange("(p t) k -> p t k", t=TILES))
-        w_stage = [None] * BLOCKS
+        def block_cols(j):
+            return slice(j * BANK, (j + 1) * BANK)
 
-        def load_w(c):
-            w_stage[c] = stage_tile()
-            nc.sync.dma_start(out=w_stage[c][:], in_=w_hh1[c * BANK:(c + 1) * BANK, :].rearrange("(b p) k -> p b k", p=P))
+        def gate_cols(gate):
+            return slice(gate * H, (gate + 1) * H)
 
-        load_w(0)
-        make_identity(nc, ident_bf16[:])
-        nc.gpsimd.memset(vec_rows[3 * CHUNKS:, :], 0.0)
-        make_identity(nc, ident_f32[:])
-        nc.gpsimd.memset(neg_half[:], -0.5)
+        def r_cols(t, cols):
+            return r_pair[t // 2][:, t % 2, cols]
 
-        def transpose_words(stage, q, banks):
-            tiles = []
-            for hb in range(2):
-                bk = bank(banks[hb])
-                view = bk[:].rearrange("p (b w r) -> p b w r", b=2, w=2)
-                for b in range(2):
-                    words = stage[:, 2 * hb + b, :].bitcast(F32)
-                    for w in range(2):
-                        nc.tensor.transpose(view[:, b, w, :], words[:, 256 * q + w:256 * (q + 1):2], ident_f32[:])
-                tiles.append(bk)
-            return tiles
-
-        def new_grouped():
-            return shared.tile([P, 4 * BANK], BF16, name="grouped", tag="grouped", bufs=3, align_bytes=64,
-                               offset=STAGE_BUFS * 4 * H * 2)
-
-        def interleave(engine, grouped, hb, bk):
-            dst = grouped[:].bitcast(F32)[:, hb * BANK:(hb + 1) * BANK].rearrange("p (b r w) -> p b r w", b=2, w=2)
-            src = bk[:].rearrange("p (b w r) -> p b r w", b=2, w=2)
-            if engine == "vector":
-                nc.vector.tensor_copy(out=dst, in_=src)
-            else:
-                nc.scalar.copy(out=dst, in_=src)
-
-        def quantize(grouped, codes, scales):
-            nc.vector.quantize_mx(out=codes.bitcast(FP8X4), scales=scales, in_=grouped[:])
-
-        def discard():
-            return keep.tile([P, BANK], BF16, name="discard", tag="discard", bufs=3)
-
-        def a_matmul(t, j, i):
-            bk = bank(i)
-            nc.tensor.matmul(bk[:], lhsT=x_t[:, t * P:(t + 1) * P], rhs=wih_t[:, j * BANK:(j + 1) * BANK], start=True, stop=True)
-            return bk
-
-        def a_square(t, j, bk):
-            sq = discard()
-            nc.scalar.activation(out=sq[:], in_=bk[:], func=ACT.Square, bias=neg_mu_a[:, t:t + 1], accum_out=ssq_a[:, t, j:j + 1])
-
-        def a_gain(t, j, bk):
-            cols = slice(j * BANK, (j + 1) * BANK)
-            nc.vector.scalar_tensor_tensor(out=u[:, t, cols], in0=bk[:], scalar=neg_mu_a[:, t:t + 1], in1=gain_i[:, cols],
-                                           op0=ALU.add, op1=ALU.mult)
+        def inverse_root(var, name):
+            rstd = small(name, var.shape[1])
+            nc.gpsimd.tensor_tensor(out=rstd[:], in0=var, in1=neg_half[:, :var.shape[1]], op=ALU.pow)
+            return rstd
 
         def r_matmul(t, j, i):
             bk = bank(i)
@@ -152,266 +109,242 @@ def tile_multilstm_pa_kernel(tc, x, h0, c0, w_ih1, w_hh1, lni_w1, lni_b1, lnh_w1
                                     start=(q == 0), stop=(q == PASSES - 1))
             return bk
 
-        def r_cols(t, cols):
-            return r_pairs[t // 2][:, t % 2, cols]
-
         def r_copy(t, j, bk):
-            nc.scalar.activation(out=r_cols(t, slice(j * BANK, (j + 1) * BANK)), in_=bk[:], func=ACT.Copy,
-                                 accum_out=sums_r[:, 0, t, j:j + 1])
-
-        def r_shift(t):
-            nc.scalar.activation(out=neg_shift[:, t:t + 1], in_=sums_r[:, 0, t, 0:1], func=ACT.Copy, scale=-1.0 / BANK)
+            nc.scalar.activation(out=r_cols(t, block_cols(j)), in_=bk[:], func=ACT.Copy, accum_out=sums_r[:, 0, t, j:j + 1])
 
         def r_square(t, j):
-            sq = discard()
-            nc.scalar.activation(out=sq[:], in_=r_cols(t, slice(j * BANK, (j + 1) * BANK)), func=ACT.Square,
+            squares = discard()
+            nc.scalar.activation(out=squares[:], in_=r_cols(t, block_cols(j)), func=ACT.Square,
                                  bias=neg_shift[:, t:t + 1], accum_out=sums_r[:, 1, t, j:j + 1])
 
-        def small(name, width):
-            return keep.tile([P, width], F32, name=name, tag=name, bufs=3)
-
-        def rstd_a(pair):
+        def a_rstd(pair):
             total = small("a_total", 2)
             nc.vector.tensor_reduce(out=total[:], in_=ssq_a[:, 2 * pair:2 * pair + 2, :], axis=AXIS.X, op=ALU.add)
             var = small("a_var", 2)
             nc.vector.tensor_scalar(out=var[:], in0=total[:], scalar1=1.0 / G, scalar2=EPS, op0=ALU.mult, op1=ALU.add)
-            rstd = small("a_rstd", 2)
-            nc.gpsimd.tensor_tensor(out=rstd[:], in0=var[:], in1=neg_half[:], op=ALU.pow)
-            return rstd
+            rstd_a.append(inverse_root(var[:], "a_rstd"))
 
-        def scale_u(t, cols, rstd, engine=SCALE_U):
-            if engine == "scalar":
-                nc.scalar.activation(out=u[:, t, cols], in_=u[:, t, cols], func=ACT.Copy, scale=rstd[:, t % 2:t % 2 + 1])
-            elif engine == "vector":
-                nc.vector.tensor_scalar(out=u[:, t, cols], in0=u[:, t, cols], scalar1=rstd[:, t % 2:t % 2 + 1], scalar2=None, op0=ALU.mult)
+        def scale(ap, factor, engine):
+            if engine == "vector":
+                nc.vector.tensor_scalar(out=ap, in0=ap, scalar1=factor, scalar2=None, op0=ALU.mult)
+            elif engine == "gpsimd":
+                nc.gpsimd.tensor_scalar(out=ap, in0=ap, scalar1=factor, scalar2=0.0, op0=ALU.mult, op1=ALU.add)
             else:
-                nc.gpsimd.tensor_scalar(out=u[:, t, cols], in0=u[:, t, cols], scalar1=rstd[:, t % 2:t % 2 + 1], scalar2=0.0,
-                                        op0=ALU.mult, op1=ALU.add)
+                nc.scalar.activation(out=ap, in_=ap, func=ACT.Copy, scale=factor)
 
-        x_bank = bank(0, BF16)
-        for t in range(TILES):
-            nc.tensor.transpose(x_bank[:, t * P:(t + 1) * P], x_rows[:, t, :], ident_bf16[:])
-        nc.vector.tensor_copy(out=x_t[:], in_=x_bank[:, :B])
-        nc.vector.tensor_copy(out=x_t32[:], in_=x_bank[:, :B])
+        def scale_u(t, cols, engine):
+            scale(u[:, t, cols], rstd_a[t // 2][:, t % 2:t % 2 + 1], engine)
 
-        def gain_bank(k, i):
-            bk = bank(i, BF16)
-            for c in range(8):
-                nc.tensor.matmul(bk[:, c * P:(c + 1) * P], lhsT=ident_bf16[:, 8 * k + c:8 * k + c + 1].to_broadcast([P, P]),
-                                 rhs=vec_rows[:], start=True, stop=True)
-            return bk
+        def stream_weights():
+            for k, vec in enumerate((lni_w1, lni_b1, lnh_b1)):
+                nc.scalar.dma_start(out=vec_rows[k * CHUNKS:(k + 1) * CHUNKS, :], in_=vec.rearrange("(c p) -> c p", p=P))
+            nc.sync.dma_start(out=x_rows[:], in_=x.rearrange("(p t) v -> p t v", t=TILES))
+            wih_stage = stage_tile()
+            wih_rows = wih_stage[:].rearrange("p b (j c v) -> p (b j) c v", c=4, v=V)
+            for k in range(4):
+                nc.sync.dma_start(out=wih_rows[:, 2 * k:2 * (k + 1), :, :],
+                                  in_=w_ih1[gate_cols(k), :].rearrange("(j p c) v -> p j c v", p=P, c=4))
+            h_stage = stage_tile()
+            nc.sync.dma_start(out=h_stage[:], in_=h0.rearrange("(p t) k -> p t k", t=TILES))
+            w_stage = []
 
-        def wih_bank(k, i):
-            bk = bank(i, BF16)
-            for jc in range(8):
-                nc.tensor.transpose(bk[:, jc * P:(jc + 1) * P], wih_rows[:, 2 * k + jc // 4, jc % 4, :], ident_bf16[:])
-            dst = wih_t[:, 2 * k * BANK:2 * (k + 1) * BANK].rearrange("p (j r c) -> p j r c", j=2, c=4)
-            src = bk[:].rearrange("p (j c r) -> p j r c", j=2, c=4)
-            if k % 2 == 0:
-                nc.scalar.activation(out=dst, in_=src, func=ACT.Copy, accum_out=wih_sums[:, k:k + 1])
-            else:
-                nc.vector.tensor_scalar(out=dst, in0=src, scalar1=1.0, scalar2=None, op0=ALU.mult, op1=ALU.add, accum_out=wih_sums[:, k:k + 1])
+            def load_w():
+                rows = w_hh1[block_cols(len(w_stage)), :]
+                w_stage.append(stage_tile())
+                nc.sync.dma_start(out=w_stage[-1][:], in_=rows.rearrange("(b p) k -> p b k", p=P))
 
-        def gain_part(k, i):
-            bk = gain_bank(k, i)
-            cols = slice(2 * k * BANK, 2 * (k + 1) * BANK)
-            if k % 2 == 1:
-                nc.scalar.copy(out=gain_i[:, cols], in_=bk[:])
-            else:
-                nc.vector.tensor_copy(out=gain_i[:, cols], in_=bk[:])
+            load_w()
+            make_identity(nc, ident_bf16[:])
+            nc.gpsimd.memset(vec_rows[3 * CHUNKS:, :], 0.0)
+            make_identity(nc, ident_f32[:])
+            nc.gpsimd.memset(neg_half[:], -0.5)
 
-        for k in range(4):
-            wih_bank(k, 1 + k)
-            gain_part(k, (5, 6, 7, 0)[k])
-        scaled_sums = small("scaled_sums", 4)
-        nc.vector.tensor_scalar(out=scaled_sums[:], in0=wih_sums[:], scalar1=-1.0 / G, scalar2=None, op0=ALU.mult, op1=ALU.add,
-                                accum_out=neg_wbar[:])
-        load_w(1)
+            x_bank = bank(0, BF16)
+            for t in range(TILES):
+                nc.tensor.transpose(x_bank[:, t * P:(t + 1) * P], x_rows[:, t, :], ident_bf16[:])
+            nc.vector.tensor_copy(out=x_t[:], in_=x_bank[:, :B])
+            nc.vector.tensor_copy(out=x_t32[:], in_=x_bank[:, :B])
 
-        steps = PASSES + BLOCKS * PASSES
-        a_units = [(t, j) for t in range(TILES) for j in range(BLOCKS)]
-        groupeds = {}
-        rstds_a = {}
-        next_bank = [0]
-
-        def rolling():
-            next_bank[0] += 1
-            return 4 + next_bank[0] % 4
-
-        for s in range(steps + 1):
-            c, q = divmod(s - PASSES, PASSES)
-            units = []
-            for k in range(A_PER_STEP[s]):
-                t, j = a_units.pop(0)
-                units.append((t, j, a_matmul(t, j, rolling())))
-            r_unit = None
-            if PASSES + 3 <= s:
-                j, t = divmod(s - PASSES - 3, 2)
-                r_unit = (t, j, r_matmul(t, j, rolling()))
-            t_tiles = None
-            if s < steps:
-                t_tiles = transpose_words(h_stage if c < 0 else w_stage[c], q, (2 * q, 2 * q + 1))
-                groupeds[s] = new_grouped()
-                if q == PASSES - 1 and c + STAGE_BUFS < BLOCKS:
-                    load_w(c + STAGE_BUFS)
-                if q == PASSES - 1 and c + STAGE_BUFS == BLOCKS:
-                    nc.sync.dma_start(out=gain_h[:], in_=lnh_w1.partition_broadcast(P))
-                    nc.sync.dma_start(out=c_rows[:], in_=c0.rearrange("(p t) h -> p t h", t=TILES))
-                    nc.sync.dma_start(out=gain_c[:], in_=lnc_w1.partition_broadcast(P))
-                    nc.sync.dma_start(out=bias_c[:], in_=lnc_b1.partition_broadcast(P))
-            if len(units) == 2:
-                a_square(*units[0])
-                a_gain(*units[1])
-                a_gain(*units[0])
-                a_square(*units[1])
-            if len(units) == 1:
-                a_gain(*units[0])
-            if r_unit is not None:
-                r_copy(*r_unit)
-            if len(units) == 1:
-                a_square(*units[0])
-            if 1 <= s <= steps:
-                cq, qq = divmod(s - 1 - PASSES, PASSES)
-                if cq < 0:
-                    quantize(groupeds[s - 1], h_codes[:, qq, :], h_scales[:, qq, :])
+            def spread_gain(k, i):
+                bk = bank(i, BF16)
+                for c in range(8):
+                    nc.tensor.matmul(bk[:, c * P:(c + 1) * P], lhsT=ident_bf16[:, 8 * k + c:8 * k + c + 1].to_broadcast([P, P]),
+                                     rhs=vec_rows[:], start=True, stop=True)
+                if k % 2 == 1:
+                    nc.scalar.copy(out=gain_i[:, gate_cols(k)], in_=bk[:])
                 else:
-                    quantize(groupeds[s - 1], w_codes[:, cq, qq, :], w_scales[:, cq, qq, :])
-            if PASSES + 4 <= s:
-                j, t = divmod(s - PASSES - 4, 2)
-                r_square(t, j)
-            if r_unit is not None and r_unit[1] == 0:
-                r_shift(r_unit[0])
-            if t_tiles is not None:
-                on_scalar = SCALAR_COPIES[s]
-                interleave("scalar" if on_scalar == 2 else "vector", groupeds[s], 0, t_tiles[0])
-                interleave("scalar" if on_scalar >= 1 else "vector", groupeds[s], 1, t_tiles[1])
-            if s == 0:
-                mu_bank = bank(rolling())
-                for t in range(TILES):
-                    nc.tensor.matmul(mu_bank[:, t:t + 1], lhsT=x_t32[:, t * P:(t + 1) * P], rhs=neg_wbar[:], start=True, stop=True)
-                nc.vector.tensor_copy(out=neg_mu_a[:], in_=mu_bank[:, :TILES])
-            if s == 4:
-                bias_bank = bank(rolling(), BF16)
-                nc.tensor.transpose(bias_bank[:, :P], vec_rows[:], ident_bf16[:])
-                nc.scalar.copy(out=bias_i[:], in_=bias_bank[:, CHUNKS:2 * CHUNKS])
-                nc.vector.tensor_tensor(out=bias[:], in0=bias_bank[:, 2 * CHUNKS:3 * CHUNKS], in1=bias_i[:], op=ALU.add)
-            if s == RSTD_A_STEP:
-                rstds_a[0] = rstd_a(0)
-            if RSTD_A_STEP < s <= RSTD_A_STEP + 8:
-                k = s - RSTD_A_STEP - 1
-                scale_u(k % 2, slice((k // 2) * H, (k // 2 + 1) * H), rstds_a[0])
+                    nc.vector.tensor_copy(out=gain_i[:, gate_cols(k)], in_=bk[:])
 
-        r_pairs[1] = shared.tile([P, 2, G], F32, name="r_second", tag="r_second", align_bytes=64, offset=0)
+            def transpose_wih(k, i):
+                bk = bank(i, BF16)
+                for jc in range(8):
+                    nc.tensor.transpose(bk[:, jc * P:(jc + 1) * P], wih_rows[:, 2 * k + jc // 4, jc % 4, :], ident_bf16[:])
+                dst = wih_t[:, gate_cols(k)].rearrange("p (j r c) -> p j r c", j=2, c=4)
+                src = bk[:].rearrange("p (j c r) -> p j r c", j=2, c=4)
+                if k % 2 == 0:
+                    nc.scalar.activation(out=dst, in_=src, func=ACT.Copy, accum_out=wih_sums[:, k:k + 1])
+                else:
+                    nc.vector.tensor_scalar(out=dst, in0=src, scalar1=1.0, scalar2=None, op0=ALU.mult, op1=ALU.add,
+                                            accum_out=wih_sums[:, k:k + 1])
 
-        def stats_r(group, fill_1, fill_2):
-            n = len(group)
-            tiles = slice(group[0], group[0] + n)
-            total = small("r_total", 4)
-            nc.vector.tensor_reduce(out=total[:, :2 * n].rearrange("p (k t) -> p k t", k=2), in_=sums_r[:, :, tiles, :], axis=AXIS.X, op=ALU.add)
-            fill_1()
-            nc.vector.tensor_scalar(out=neg_mu_r[:, tiles], in0=total[:, :n], scalar1=-1.0 / G, scalar2=None, op0=ALU.mult)
-            parts = small("r_parts", 6)
-            nc.vector.scalar_tensor_tensor(out=parts[:, 0:n], in0=total[:, :n], scalar=1.0 / G, in1=neg_shift[:, tiles], op0=ALU.mult, op1=ALU.add)
-            nc.vector.scalar_tensor_tensor(out=parts[:, 2:2 + n], in0=total[:, :n], scalar=-1.0 / G, in1=neg_shift[:, tiles], op0=ALU.mult, op1=ALU.subtract)
-            nc.vector.tensor_scalar(out=parts[:, 4:4 + n], in0=total[:, n:2 * n], scalar1=1.0 / G, scalar2=EPS, op0=ALU.mult, op1=ALU.add)
-            fill_2()
-            var = small("r_var", 2)
-            for k in range(n):
-                nc.vector.scalar_tensor_tensor(out=var[:, k:k + 1], in0=parts[:, k:k + 1], scalar=parts[:, 2 + k:3 + k], in1=parts[:, 4 + k:5 + k],
-                                               op0=ALU.mult, op1=ALU.add)
-            rstd = small("r_rstd", 2)
-            nc.gpsimd.tensor_tensor(out=rstd[:, :n], in0=var[:, :n], in1=neg_half[:, :n], op=ALU.pow)
-            for k, t in enumerate(group):
-                rstd_r[t] = rstd[:, k:k + 1]
+            spread_gain(0, 5)
+            for k in range(4):
+                transpose_wih(k, 1 + k)
+            scaled_sums = small("scaled_sums", 4)
+            nc.vector.tensor_scalar(out=scaled_sums[:], in0=wih_sums[:], scalar1=-1.0 / G, scalar2=None, op0=ALU.mult, op1=ALU.add,
+                                    accum_out=neg_wbar[:])
+            load_w()
+            mu_bank = bank(6)
+            for t in range(TILES):
+                nc.tensor.matmul(mu_bank[:, t:t + 1], lhsT=x_t32[:, t * P:(t + 1) * P], rhs=neg_wbar[:], start=True, stop=True)
+            nc.vector.tensor_copy(out=neg_mu_a[:], in_=mu_bank[:, :TILES])
+            for k in range(1, 4):
+                spread_gain(k, (5, 7, 5, 6)[k])
 
-        rstd_r = {}
+            def transpose_words(stage, q):
+                banks = []
+                for half in range(2):
+                    bk = bank(2 * q + half)
+                    view = bk[:].rearrange("p (b w r) -> p b w r", b=2, w=2)
+                    for b in range(2):
+                        words = stage[:, 2 * half + b, :].bitcast(F32)
+                        for w in range(2):
+                            nc.tensor.transpose(view[:, b, w, :], words[:, 256 * q + w:256 * (q + 1):2], ident_f32[:])
+                    banks.append(bk)
+                return banks
 
-        def gate_cols(gate):
-            return slice(gate * H, (gate + 1) * H)
+            def interleave(grouped, half, bk, on_scalar):
+                dst = grouped[:].bitcast(F32)[:, block_cols(half)].rearrange("p (b r w) -> p b r w", b=2, w=2)
+                src = bk[:].rearrange("p (b w r) -> p b r w", b=2, w=2)
+                if on_scalar:
+                    nc.scalar.copy(out=dst, in_=src)
+                else:
+                    nc.vector.tensor_copy(out=dst, in_=src)
 
-        def r_gain(t, gate):
-            ap = r_cols(t, gate_cols(gate))
-            nc.vector.scalar_tensor_tensor(out=ap, in0=ap, scalar=neg_mu_r[:, t:t + 1], in1=gain_h[:, gate_cols(gate)],
-                                           op0=ALU.add, op1=ALU.mult)
+            def a_square(t, j, bk):
+                squares = discard()
+                nc.scalar.activation(out=squares[:], in_=bk[:], func=ACT.Square, bias=neg_mu_a[:, t:t + 1],
+                                     accum_out=ssq_a[:, t, j:j + 1])
 
-        def r_scale(t, gate, engine="vector"):
-            ap = r_cols(t, gate_cols(gate))
-            if engine == "gpsimd":
-                nc.gpsimd.tensor_scalar(out=ap, in0=ap, scalar1=rstd_r[t], scalar2=0.0, op0=ALU.mult, op1=ALU.add)
-            elif engine == "vector":
-                nc.vector.tensor_scalar(out=ap, in0=ap, scalar1=rstd_r[t], scalar2=None, op0=ALU.mult)
-            else:
-                nc.scalar.activation(out=ap, in_=ap, func=ACT.Copy, scale=rstd_r[t])
+            def a_gain(t, j, bk):
+                nc.vector.scalar_tensor_tensor(out=u[:, t, block_cols(j)], in0=bk[:], scalar=neg_mu_a[:, t:t + 1],
+                                               in1=gain_i[:, block_cols(j)], op0=ALU.add, op1=ALU.mult)
 
-        def gate_sum(pair, gate, k, i):
-            bk = bank(i)
-            view = bk[:].rearrange("p (c t b) -> p c t b", c=2, t=2)
-            for cc in range(2):
-                chunk = gate * 8 + 2 * k + cc
-                cols = slice(chunk * P, (chunk + 1) * P)
-                for tt in range(2):
-                    t = 2 * pair + tt
-                    nc.tensor.matmul(view[:, cc, tt, :], lhsT=u[:, t, cols], rhs=ident_f32[:], start=True, stop=False, is_transpose=True)
-                    nc.tensor.matmul(view[:, cc, tt, :], lhsT=r_cols(t, cols), rhs=ident_f32[:], start=False, stop=True, is_transpose=True)
-            for cc in range(2):
-                chunk = gate * 8 + 2 * k + cc
-                nc.scalar.activation(out=r_pairs[pair][:, :, chunk * P:(chunk + 1) * P], in_=view[:, cc, :, :],
-                                     func=ACT.Tanh if gate == GATE_G else ACT.Sigmoid, bias=bias[:, chunk:chunk + 1])
+            taken = [0]
 
-        gate_count = [0]
+            def rolling():
+                taken[0] += 1
+                return 4 + taken[0] % 4
 
-        def gate_half(pair, gate, half, banks=(0, 1, 2)):
-            for k in (2 * half, 2 * half + 1):
-                gate_count[0] += 1
-                gate_sum(pair, gate, k, banks[gate_count[0] % len(banks)])
+            grouped = []
+            for s in range(STEPS + 1):
+                c, q = divmod(s - PASSES, PASSES)
+                a_units = []
+                if 1 <= s <= TILES * BLOCKS // 2:
+                    for k in range(2):
+                        t, j = divmod(2 * (s - 1) + k, BLOCKS)
+                        bk = bank(rolling())
+                        nc.tensor.matmul(bk[:], lhsT=x_t[:, t * P:(t + 1) * P], rhs=wih_t[:, block_cols(j)], start=True, stop=True)
+                        a_units.append((t, j, bk))
+                r_j, r_t = divmod(s - PASSES - 3, 2)
+                if r_j >= 0:
+                    r_bank = r_matmul(r_t, r_j, rolling())
+                if s < STEPS:
+                    word_banks = transpose_words(h_stage if c < 0 else w_stage[c], q)
+                    grouped.append(grouped_tile())
+                    if q == PASSES - 1 and len(w_stage) < BLOCKS:
+                        load_w()
+                    if q == PASSES - 1 and c + STAGE_BUFS == BLOCKS:
+                        nc.sync.dma_start(out=gain_h[:], in_=lnh_w1.partition_broadcast(P))
+                        nc.sync.dma_start(out=c_rows[:], in_=c0.rearrange("(p t) h -> p t h", t=TILES))
+                        nc.sync.dma_start(out=gain_c[:], in_=lnc_w1.partition_broadcast(P))
+                        nc.sync.dma_start(out=bias_c[:], in_=lnc_b1.partition_broadcast(P))
+                if a_units:
+                    a_square(*a_units[0])
+                    a_gain(*a_units[1])
+                    a_gain(*a_units[0])
+                    a_square(*a_units[1])
+                if r_j >= 0:
+                    r_copy(r_t, r_j, r_bank)
+                if s >= 1:
+                    last_c, last_q = divmod(s - 1 - PASSES, PASSES)
+                    codes = h_codes[:, last_q, :] if last_c < 0 else w_codes[:, last_c, last_q, :]
+                    scales = h_scales[:, last_q, :] if last_c < 0 else w_scales[:, last_c, last_q, :]
+                    nc.vector.quantize_mx(out=codes.bitcast(FP8X4), scales=scales, in_=grouped[s - 1][:])
+                if s >= PASSES + 4:
+                    r_square((s - PASSES - 4) % 2, (s - PASSES - 4) // 2)
+                if r_j == 0:
+                    nc.scalar.activation(out=neg_shift[:, r_t:r_t + 1], in_=sums_r[:, 0, r_t, 0:1], func=ACT.Copy, scale=-1.0 / BANK)
+                if s < STEPS:
+                    interleave(grouped[s], 0, word_banks[0], SCALAR_COPIES[s] == 2)
+                    interleave(grouped[s], 1, word_banks[1], SCALAR_COPIES[s] >= 1)
+                if s == 4:
+                    bias_bank = bank(rolling(), BF16)
+                    nc.tensor.transpose(bias_bank[:, :P], vec_rows[:], ident_bf16[:])
+                    nc.scalar.copy(out=bias_i[:], in_=bias_bank[:, CHUNKS:2 * CHUNKS])
+                    nc.vector.tensor_tensor(out=bias[:], in0=bias_bank[:, 2 * CHUNKS:3 * CHUNKS], in1=bias_i[:], op=ALU.add)
+                if s == FIRST_RSTD_STEP:
+                    a_rstd(0)
+                if FIRST_RSTD_STEP < s <= FIRST_RSTD_STEP + 8:
+                    k = s - FIRST_RSTD_STEP - 1
+                    scale_u(k % 2, gate_cols(k // 2), "vector")
+            a_rstd(1)
 
-        def mean_passes(t, bk, blocks):
-            rows = slice(t * P, (t + 1) * P)
-            for j in blocks:
-                for q in range(PASSES):
-                    nc.tensor.matmul_mx(out=bk[:], lhsT=h_codes[:, q, rows].bitcast(FP8X4), lhsT_scale=h_scales[:, q, rows],
-                                        rhs=w_codes[:, j, q, :].bitcast(FP8X4), rhs_scale=w_scales[:, j, q, :],
-                                        start=(j == 0 and q == 0), stop=(j == BLOCKS - 1 and q == PASSES - 1))
+        with tc.manual_schedule(engines={ENGINE.SP}):
+            stream_weights()
 
-        def mean_read(t, bk):
-            sq = discard()
-            nc.scalar.activation(out=sq[:], in_=bk[:], func=ACT.Copy, scale=-1.0 / G, accum_out=neg_mu_r[:, t:t + 1])
+        ctx.enter_context(tc.manual_schedule(engines={ENGINE.SP}))
+        r_pair.append(shared.tile([P, 2, G], F32, name="r_second", tag="r_second", align_bytes=64, offset=0))
+        neg_mu_r = small("neg_mu_r", 2)
+        late = {}
 
-        late_tiles = {}
+        def first_round(n, i):
+            j, tt = divmod(n, 2)
+            bk = r_matmul(2 + tt, j, i)
+            return lambda: nc.vector.bn_stats(out=bn_r[:, tt, j, :], in_=bk[:])
 
-        def late_matmul(t, j):
-            late_tiles[(t, j)] = r_matmul(t, j, LATE_BANKS[j % len(LATE_BANKS)])
+        def gate_block(pair, j, banks):
+            gate = j // 2
+            for half in range(2):
+                bk = bank(banks[half])
+                view = bk[:].rearrange("p (c t b) -> p c t b", c=2, t=2)
+                chunks = [4 * j + 2 * half + cc for cc in range(2)]
+                for cc, chunk in enumerate(chunks):
+                    cols = slice(chunk * P, (chunk + 1) * P)
+                    for tt in range(2):
+                        t = 2 * pair + tt
+                        nc.tensor.matmul(view[:, cc, tt, :], lhsT=u[:, t, cols], rhs=ident_f32[:], start=True, stop=False,
+                                         is_transpose=True)
+                        nc.tensor.matmul(view[:, cc, tt, :], lhsT=r_cols(t, cols), rhs=ident_f32[:], start=False, stop=True,
+                                         is_transpose=True)
+                for cc, chunk in enumerate(chunks):
+                    nc.scalar.activation(out=r_pair[pair][:, :, chunk * P:(chunk + 1) * P], in_=view[:, cc, :, :],
+                                         func=ACT.Tanh if gate == GATE_G else ACT.Sigmoid, bias=bias[:, chunk:chunk + 1])
 
-        def late_square(t, j):
-            sq = discard()
-            nc.scalar.activation(out=sq[:], in_=late_tiles[(t, j)][:], func=ACT.Square, bias=neg_mu_r[:, t:t + 1],
-                                 accum_out=sums_r[:, 1, t, j:j + 1])
+        def centre_first(j):
+            for t in range(2):
+                ap = r_cols(t, block_cols(j))
+                nc.vector.scalar_tensor_tensor(out=ap, in0=ap, scalar=neg_mu_r[:, t:t + 1], in1=gain_h[:, block_cols(j)],
+                                               op0=ALU.add, op1=ALU.mult)
 
-        def late_gain(t, j):
-            cols = slice(j * BANK, (j + 1) * BANK)
-            nc.vector.scalar_tensor_tensor(out=r_cols(t, cols), in0=late_tiles[(t, j)][:], scalar=neg_mu_r[:, t:t + 1], in1=gain_h[:, cols],
-                                           op0=ALU.add, op1=ALU.mult)
+        def scale_first(j, engine):
+            for t in range(2):
+                scale(r_cols(t, block_cols(j)), late["rstd_first"][:, t:t + 1], engine)
 
-        def late(t, j):
-            late_matmul(t, j)
-            late_square(t, j)
-            late_gain(t, j)
+        def second_round(j):
+            for tt in range(2):
+                nc.scalar.activation(out=r_cols(2 + tt, block_cols(j)), in_=r_matmul(2 + tt, j, 3 + tt)[:], func=ACT.Identity,
+                                     scale=late["rstd_second"][:, tt:tt + 1], bias=late["offset"][:, tt:tt + 1])
 
-        def sum_blocks(parts):
-            total = small("total", 2)
-            nc.vector.tensor_reduce(out=total[:], in_=parts, axis=AXIS.X, op=ALU.add)
-            return total
+        def gain_second(j):
+            both = r_pair[1][:, :, block_cols(j)]
+            nc.vector.tensor_tensor(out=both, in0=both, in1=gain_h[:, block_cols(j)].unsqueeze(1).to_broadcast([P, 2, BANK]),
+                                    op=ALU.mult)
 
-        def rstd_from(total):
-            var = small("var", 2)
-            nc.vector.tensor_scalar(out=var[:], in0=total[:], scalar1=1.0 / G, scalar2=EPS, op0=ALU.mult, op1=ALU.add)
-            rstd = small("rstd", 2)
-            nc.gpsimd.tensor_tensor(out=rstd[:], in0=var[:], in1=neg_half[:], op=ALU.pow)
-            return rstd
-
-        def input_times_cell(t):
+        def input_times_cell(t, engine="vector"):
             ap = r_cols(t, gate_cols(GATE_I))
-            nc.vector.tensor_tensor(out=ap, in0=ap, in1=r_cols(t, gate_cols(GATE_G)), op=ALU.mult)
+            eng = nc.vector if engine == "vector" else nc.gpsimd
+            eng.tensor_tensor(out=ap, in0=ap, in1=r_cols(t, gate_cols(GATE_G)), op=ALU.mult)
 
         def c0_transposed(t, i):
             bk = bank(i, BF16)
@@ -428,9 +361,9 @@ def tile_multilstm_pa_kernel(tc, x, h0, c0, w_ih1, w_hh1, lni_w1, lni_b1, lnh_w1
             for half in range(2):
                 bk = bank(banks[half])
                 for jj in range(4):
-                    j = 4 * half + jj
+                    first = (4 * half + jj) * P
                     for k, gate in enumerate(gates):
-                        nc.tensor.matmul(bk[:, jj * P:(jj + 1) * P], lhsT=r_cols(t, slice(gate * H + j * P, gate * H + (j + 1) * P)),
+                        nc.tensor.matmul(bk[:, jj * P:(jj + 1) * P], lhsT=r_cols(t, slice(gate * H + first, gate * H + first + P)),
                                          rhs=ident_f32[:], start=(k == 0), stop=(k == len(gates) - 1), is_transpose=True)
                 tiles.append(bk)
             return tiles
@@ -449,19 +382,16 @@ def tile_multilstm_pa_kernel(tc, x, h0, c0, w_ih1, w_hh1, lni_w1, lni_b1, lnh_w1
         def cell_rstd(mean_var):
             var = small("c_var", 1)
             nc.vector.tensor_scalar(out=var[:], in0=mean_var[:, 1:2], scalar1=EPS, scalar2=None, op0=ALU.add)
-            rstd = small("c_rstd", 1)
-            nc.gpsimd.tensor_tensor(out=rstd[:], in0=var[:], in1=neg_half[:, 0:1], op=ALU.pow)
-            return mean_var, rstd
+            return inverse_root(var[:], "c_rstd")
 
-        def cell_centre(t, tiles, stats):
+        def cell_centre(t, tiles, mean_var):
             for half in range(2):
-                cols = slice(half * BANK, (half + 1) * BANK)
-                nc.vector.scalar_tensor_tensor(out=u[:, t, cols], in0=tiles[half][:], scalar=stats[0][:, 0:1], in1=gain_c[:, cols],
-                                               op0=ALU.subtract, op1=ALU.mult)
+                nc.vector.scalar_tensor_tensor(out=u[:, t, block_cols(half)], in0=tiles[half][:], scalar=mean_var[:, 0:1],
+                                               in1=gain_c[:, block_cols(half)], op0=ALU.subtract, op1=ALU.mult)
 
-        def cell_finish(t, stats):
+        def cell_finish(t, rstd):
             cy = u[:, t, 0:H]
-            nc.vector.scalar_tensor_tensor(out=cy, in0=cy, scalar=stats[1][:, 0:1], in1=bias_c[:], op0=ALU.mult, op1=ALU.add)
+            nc.vector.scalar_tensor_tensor(out=cy, in0=cy, scalar=rstd[:], in1=bias_c[:], op0=ALU.mult, op1=ALU.add)
             nc.sync.dma_start(out=out_1.rearrange("(p t) h -> p t h", t=TILES)[:, t, :], in_=cy)
 
         def cell_tanh(t):
@@ -473,96 +403,145 @@ def tile_multilstm_pa_kernel(tc, x, h0, c0, w_ih1, w_hh1, lni_w1, lni_b1, lnh_w1
                 nc.vector.tensor_tensor(out=ap, in0=tiles[half][:], in1=ap, op=ALU.mult)
             nc.sync.dma_start(out=out_0.rearrange("(p t) h -> p t h", t=TILES)[:, t, :], in_=u[:, t, H:2 * H])
 
-        def prepare(group, gate, engine="vector"):
-            for t in group:
-                r_gain(t, gate)
-            for t in group:
-                r_scale(t, gate, engine)
-
-        def nothing():
-            return None
-
         last = BLOCKS - 1
         r_last = [r_matmul(t, last, 4 + t) for t in range(2)]
+        reads = [first_round(n, (0, 1, 2, 3, 6, 7)[n]) for n in range(6)]
         r_copy(0, last, r_last[0])
         r_square(1, last - 1)
         r_copy(1, last, r_last[1])
         r_square(0, last)
         r_square(1, last)
-        stats_r((0, 1), nothing, nothing)
-        mean_bank = bank(4)
-        mean_passes(2, mean_bank, range(BLOCKS))
-        mean_read(2, mean_bank)
-        for k, (t, j) in enumerate(a_units):
-            bk = a_matmul(t, j, (0, 1, 2, 3, 6, 7)[k % 6])
-            a_gain(t, j, bk)
-            a_square(t, j, bk)
-        rstds_a[1] = rstd_from(sum_blocks(ssq_a[:, 2:4, :]))
-        order = (GATE_I, GATE_G, GATE_F, GATE_O)
-        mean_bank = bank(5)
-        for n in range(4):
-            prepare((0, 1), order[n], ("vector", "vector", "vector", "vector")[n])
-            late(2, 2 * n)
-            gate_half(0, order[n], 0)
-            late(2, 2 * n + 1)
-            gate_half(0, order[n], 1)
-            if n < 2:
-                mean_passes(3, mean_bank, range(4 * n, 4 * n + 4))
+        for read in reads[:4]:
+            read()
+        total = small("r_total", 4)
+        nc.vector.tensor_reduce(out=total[:].rearrange("p (k t) -> p k t", k=2), in_=sums_r[:], axis=AXIS.X, op=ALU.add)
+        reads[4]()
+        nc.vector.tensor_scalar(out=neg_mu_r[:], in0=total[:, 0:2], scalar1=-1.0 / G, scalar2=None, op0=ALU.mult)
+        parts = small("r_parts", 6)
+        nc.vector.scalar_tensor_tensor(out=parts[:, 0:2], in0=total[:, 0:2], scalar=1.0 / G, in1=neg_shift[:], op0=ALU.mult, op1=ALU.add)
+        nc.vector.scalar_tensor_tensor(out=parts[:, 2:4], in0=total[:, 0:2], scalar=-1.0 / G, in1=neg_shift[:], op0=ALU.mult,
+                                       op1=ALU.subtract)
+        nc.vector.tensor_scalar(out=parts[:, 4:6], in0=total[:, 2:4], scalar1=1.0 / G, scalar2=EPS, op0=ALU.mult, op1=ALU.add)
+        centre_first(0)
+        var = small("r_var", 2)
+        for t in range(2):
+            nc.vector.scalar_tensor_tensor(out=var[:, t:t + 1], in0=parts[:, t:t + 1], scalar=parts[:, 2 + t:3 + t],
+                                           in1=parts[:, 4 + t:5 + t], op0=ALU.mult, op1=ALU.add)
+        late["rstd_first"] = inverse_root(var[:], "r_rstd")
+        for t in (2, 3):
+            scale_u(t, gate_cols(GATE_I), "scalar")
+        reads[5]()
+        reads = [first_round(6 + n, 3 + n) for n in range(2)]
+        reads[0]()
+        scale_first(0, "vector")
+        reads[1]()
+
+        early = [2 * gate + half for gate in (GATE_I, GATE_G, GATE_F) for half in range(2)]
+        turn = [0]
+
+        def gate_banks():
+            turn[0] += 2
+            return (turn[0] % 3, (turn[0] + 1) % 3)
+
+        for n, j in enumerate(early):
+            if n + 1 < len(early):
+                centre_first(early[n + 1])
+            gate_block(0, j, gate_banks())
+            if n < 4:
+                reads = [first_round(8 + 2 * n + k, 3 + k) for k in range(2)]
+            if n + 1 < len(early):
+                scale_first(early[n + 1], "vector")
+            if n < 4:
+                for read in reads:
+                    read()
+            if n < 4:
+                scale_u(2 + n % 2, gate_cols((GATE_G, GATE_F)[n // 2]), "scalar")
+            if n == 3:
+                mean_var = small("r_mean_var", 4)
+                for tt in range(2):
+                    nc.vector.bn_aggr(out=mean_var[:, 2 * tt:2 * tt + 2], in_=bn_r[:, tt, :, :].rearrange("p j s -> p (j s)"))
+                c0_banks = [c0_transposed(t, 5 + t) for t in range(2)]
+            if n == 4:
+                var = small("r_var", 2)
+                nc.vector.tensor_scalar(out=var[:], in0=mean_var[:, 1::2], scalar1=EPS, scalar2=None, op0=ALU.add)
+                late["rstd_second"] = inverse_root(var[:], "r_rstd")
+                input_times_cell(0)
+                late["offset"] = small("r_offset", 2)
+                nc.vector.scalar_tensor_tensor(out=late["offset"][:], in0=mean_var[:, 0::2], scalar=-1.0, in1=late["rstd_second"][:],
+                                               op0=ALU.mult, op1=ALU.mult)
+                second_round(early[0])
+                input_times_cell(1)
+        second_round(early[1])
+        gain_second(early[0])
+        forget_times_c0(0, c0_banks[0])
+        forget_times_c0(1, c0_banks[1])
+        cells = {}
+        means = {}
+        rstds = {}
+        for n, j in enumerate(early):
+            if n + 1 < len(early):
+                gain_second(early[n + 1])
+            gate_block(1, j, gate_banks())
+            if n + 2 < len(early):
+                second_round(early[n + 2])
+            if n == 0:
+                cells[0] = back(0, (GATE_I, GATE_F), (7, 5))
+                centre_first(2 * GATE_O)
+                parts = cell_parts(cells[0])
+                scale_first(2 * GATE_O, "vector")
+                means[0] = cell_mean_var(parts)
             if n == 1:
-                mean_read(3, mean_bank)
-            if n >= 2:
-                late(3, 2 * n - 4)
-                late(3, 2 * n - 3)
+                rstds[0] = cell_rstd(means[0])
+                cell_centre(0, cells[0], means[0])
+                cells[1] = back(1, (GATE_I, GATE_F), (6, 7))
+                cell_finish(0, rstds[0])
             if n == 2:
-                c0_banks = [c0_transposed(t, 6 + t) for t in (0, 1)]
-        for j in range(4, 8):
-            late(3, j)
-        rstd = rstd_from(sum_blocks(sums_r[:, 1, 2:4, :]))
-        for t in (2, 3):
-            rstd_r[t] = rstd[:, t - 2:t - 1]
-        for t in (0, 1):
-            input_times_cell(t)
-            forget_times_c0(t, c0_banks[t])
-        cell0 = back(0, (GATE_I, GATE_F), (5, 6))
-        cell1 = back(1, (GATE_I, GATE_F), (7, 3))
-        stats0 = cell_rstd(cell_mean_var(cell_parts(cell0)))
-        stats1 = cell_rstd(cell_mean_var(cell_parts(cell1)))
-        for n in range(3):
-            for t in (2, 3):
-                scale_u(t, gate_cols(order[n]), rstds_a[1], ("vector", "vector", "vector", "vector")[n])
-                r_scale(t, order[n], ("vector", "vector", "vector", "vector")[n])
-            gate_half(1, order[n], 0)
-            gate_half(1, order[n], 1)
-        cell_centre(0, cell0, stats0)
-        cell_finish(0, stats0)
-        cell_centre(1, cell1, stats1)
-        cell_finish(1, stats1)
-        c0_banks = [c0_transposed(t, 2 + t) for t in (2, 3)]
-        for t in (2, 3):
-            input_times_cell(t)
-            forget_times_c0(t, c0_banks[t - 2])
-        cell2 = back(2, (GATE_I, GATE_F), (6, 7))
-        cell3 = back(3, (GATE_I, GATE_F), (3, 4))
-        stats2 = cell_rstd(cell_mean_var(cell_parts(cell2)))
-        stats3 = cell_rstd(cell_mean_var(cell_parts(cell3)))
-        cell_tanh(0)
+                parts = cell_parts(cells[1])
+                centre_first(2 * GATE_O + 1)
+                means[1] = cell_mean_var(parts)
+                scale_first(2 * GATE_O + 1, "vector")
+            if n == 3:
+                rstds[1] = cell_rstd(means[1])
+                cell_centre(1, cells[1], means[1])
+                cell_tanh(0)
+                for t in (2, 3):
+                    scale_u(t, gate_cols(GATE_O), "scalar")
+            if n == 4:
+                c0_banks = [c0_transposed(t, 3 + t) for t in (2, 3)]
+                cell_finish(1, rstds[1])
+                input_times_cell(2)
+            if n == 5:
+                input_times_cell(3)
+        gate_block(0, 2 * GATE_O, gate_banks())
+        second_round(2 * GATE_O)
+        forget_times_c0(2, c0_banks[0])
+        forget_times_c0(3, c0_banks[1])
+        gate_block(0, 2 * GATE_O + 1, gate_banks())
+        cells[2] = back(2, (GATE_I, GATE_F), (7, 5))
         cell_tanh(1)
-        for t in (2, 3):
-            scale_u(t, gate_cols(GATE_O), rstds_a[1], ("vector", "vector", "vector", "vector")[3])
-            r_scale(t, GATE_O, ("vector", "vector", "vector", "vector")[3])
-        o0 = back(0, (GATE_O,), (5, 0))
-        hidden(0, o0)
-        o1 = back(1, (GATE_O,), (5, 0))
-        hidden(1, o1)
-        gate_half(1, GATE_O, 0, (1, 2))
-        gate_half(1, GATE_O, 1, (1, 2))
-        cell_centre(2, cell2, stats2)
-        cell_finish(2, stats2)
+        gain_second(2 * GATE_O)
+        second_round(2 * GATE_O + 1)
+        cells[3] = back(3, (GATE_I, GATE_F), (6, 0))
+        parts = cell_parts(cells[2])
+        gain_second(2 * GATE_O + 1)
+        means[2] = cell_mean_var(parts)
+        gate_block(1, 2 * GATE_O, (1, 2))
+        parts = cell_parts(cells[3])
+        rstds[2] = cell_rstd(means[2])
+        outs0 = back(0, (GATE_O,), (3, 4))
+        cell_centre(2, cells[2], means[2])
+        means[3] = cell_mean_var(parts)
+        gate_block(1, 2 * GATE_O + 1, (1, 2))
+        cell_finish(2, rstds[2])
+        rstds[3] = cell_rstd(means[3])
         cell_tanh(2)
-        cell_centre(3, cell3, stats3)
-        cell_finish(3, stats3)
+        cell_centre(3, cells[3], means[3])
+        outs1 = back(1, (GATE_O,), (7, 5))
+        hidden(0, outs0)
+        cell_finish(3, rstds[3])
         cell_tanh(3)
-        o2 = back(2, (GATE_O,), (5, 0))
-        o3 = back(3, (GATE_O,), (1, 2))
-        hidden(2, o2)
-        hidden(3, o3)
+        outs2 = back(2, (GATE_O,), (3, 4))
+        outs3 = back(3, (GATE_O,), (6, 0))
+        hidden(1, outs1)
+        hidden(2, outs2)
+        hidden(3, outs3)

@@ -29,7 +29,7 @@ STAGE_BUFS = 3
 GROUPED_BUFS = 3
 STEPS = PASSES + BLOCKS * PASSES
 SCALAR_COPIES = (1, 1, 1, 1, 1, 0, 0, 1, 0, 1, 0, 1, 1, 0, 1, 1, 1, 1)
-FIRST_RSTD_STEP = 8
+FIRST_RSTD_STEP = 9
 
 
 def tile_multilstm_pa_kernel(tc, x, h0, c0, w_ih1, w_hh1, lni_w1, lni_b1, lnh_w1, lnh_b1, lnc_w1, lnc_b1, out_0, out_1):
@@ -117,9 +117,12 @@ def tile_multilstm_pa_kernel(tc, x, h0, c0, w_ih1, w_hh1, lni_w1, lni_b1, lnh_w1
             nc.scalar.activation(out=squares[:], in_=r_cols(t, block_cols(j)), func=ACT.Square,
                                  bias=neg_shift[:, t:t + 1], accum_out=sums_r[:, 1, t, j:j + 1])
 
-        def a_rstd(pair):
+        def a_sum(pair):
             total = small("a_total", 2)
             nc.vector.tensor_reduce(out=total[:], in_=ssq_a[:, 2 * pair:2 * pair + 2, :], axis=AXIS.X, op=ALU.add)
+            return total
+
+        def a_rstd(total):
             var = small("a_var", 2)
             nc.vector.tensor_scalar(out=var[:], in0=total[:], scalar1=1.0 / G, scalar2=EPS, op0=ALU.mult, op1=ALU.add)
             rstd_a.append(inverse_root(var[:], "a_rstd"))
@@ -135,9 +138,16 @@ def tile_multilstm_pa_kernel(tc, x, h0, c0, w_ih1, w_hh1, lni_w1, lni_b1, lnh_w1
         def scale_u(t, cols, engine):
             scale(u[:, t, cols], rstd_a[t // 2][:, t % 2:t % 2 + 1], engine)
 
+        def first_round(n, i):
+            j, tt = divmod(n, 2)
+            bk = r_matmul(2 + tt, j, i)
+            return lambda: nc.vector.bn_stats(out=bn_r[:, tt, j, :], in_=bk[:])
+
+        early_reads = []
+
         def stream_weights():
             for k, vec in enumerate((lni_w1, lni_b1, lnh_b1)):
-                nc.scalar.dma_start(out=vec_rows[k * CHUNKS:(k + 1) * CHUNKS, :], in_=vec.rearrange("(c p) -> c p", p=P))
+                nc.sync.dma_start(out=vec_rows[k * CHUNKS:(k + 1) * CHUNKS, :], in_=vec.rearrange("(c p) -> c p", p=P))
             nc.sync.dma_start(out=x_rows[:], in_=x.rearrange("(p t) v -> p t v", t=TILES))
             wih_stage = stage_tile()
             wih_rows = wih_stage[:].rearrange("p b (j c v) -> p (b j) c v", c=4, v=V)
@@ -154,23 +164,17 @@ def tile_multilstm_pa_kernel(tc, x, h0, c0, w_ih1, w_hh1, lni_w1, lni_b1, lnh_w1
                 nc.sync.dma_start(out=w_stage[-1][:], in_=rows.rearrange("(b p) k -> p b k", p=P))
 
             load_w()
-            make_identity(nc, ident_bf16[:])
             nc.gpsimd.memset(vec_rows[3 * CHUNKS:, :], 0.0)
+            make_identity(nc, ident_bf16[:])
             make_identity(nc, ident_f32[:])
             nc.gpsimd.memset(neg_half[:], -0.5)
-
-            x_bank = bank(0, BF16)
-            for t in range(TILES):
-                nc.tensor.transpose(x_bank[:, t * P:(t + 1) * P], x_rows[:, t, :], ident_bf16[:])
-            nc.vector.tensor_copy(out=x_t[:], in_=x_bank[:, :B])
-            nc.vector.tensor_copy(out=x_t32[:], in_=x_bank[:, :B])
 
             def spread_gain(k, i):
                 bk = bank(i, BF16)
                 for c in range(8):
                     nc.tensor.matmul(bk[:, c * P:(c + 1) * P], lhsT=ident_bf16[:, 8 * k + c:8 * k + c + 1].to_broadcast([P, P]),
                                      rhs=vec_rows[:], start=True, stop=True)
-                if k % 2 == 1:
+                if k < 3:
                     nc.scalar.copy(out=gain_i[:, gate_cols(k)], in_=bk[:])
                 else:
                     nc.vector.tensor_copy(out=gain_i[:, gate_cols(k)], in_=bk[:])
@@ -188,23 +192,26 @@ def tile_multilstm_pa_kernel(tc, x, h0, c0, w_ih1, w_hh1, lni_w1, lni_b1, lnh_w1
                                             accum_out=wih_sums[:, k:k + 1])
 
             spread_gain(0, 5)
+            spread_gain(1, 6)
+            x_bank = bank(0, BF16)
+            for t in range(TILES):
+                nc.tensor.transpose(x_bank[:, t * P:(t + 1) * P], x_rows[:, t, :], ident_bf16[:])
+            nc.vector.tensor_copy(out=x_t[:], in_=x_bank[:, :B])
+            nc.vector.tensor_copy(out=x_t32[:], in_=x_bank[:, :B])
+
             for k in range(4):
                 transpose_wih(k, 1 + k)
             scaled_sums = small("scaled_sums", 4)
             nc.vector.tensor_scalar(out=scaled_sums[:], in0=wih_sums[:], scalar1=-1.0 / G, scalar2=None, op0=ALU.mult, op1=ALU.add,
                                     accum_out=neg_wbar[:])
             load_w()
-            mu_bank = bank(6)
-            for t in range(TILES):
-                nc.tensor.matmul(mu_bank[:, t:t + 1], lhsT=x_t32[:, t * P:(t + 1) * P], rhs=neg_wbar[:], start=True, stop=True)
-            nc.vector.tensor_copy(out=neg_mu_a[:], in_=mu_bank[:, :TILES])
-            for k in range(1, 4):
-                spread_gain(k, (5, 7, 5, 6)[k])
+            spread_gain(2, 5)
+            spread_gain(3, 6)
 
-            def transpose_words(stage, q):
+            def transpose_words(stage, q, s):
                 banks = []
                 for half in range(2):
-                    bk = bank(2 * q + half)
+                    bk = bank((2 * s + half) % 3)
                     view = bk[:].rearrange("p (b w r) -> p b w r", b=2, w=2)
                     for b in range(2):
                         words = stage[:, 2 * half + b, :].bitcast(F32)
@@ -230,27 +237,23 @@ def tile_multilstm_pa_kernel(tc, x, h0, c0, w_ih1, w_hh1, lni_w1, lni_b1, lnh_w1
                 nc.vector.scalar_tensor_tensor(out=u[:, t, block_cols(j)], in0=bk[:], scalar=neg_mu_a[:, t:t + 1],
                                                in1=gain_i[:, block_cols(j)], op0=ALU.add, op1=ALU.mult)
 
-            taken = [0]
-
-            def rolling():
-                taken[0] += 1
-                return 4 + taken[0] % 4
-
             grouped = []
+            a_units = []
             for s in range(STEPS + 1):
                 c, q = divmod(s - PASSES, PASSES)
+                last_units = a_units
                 a_units = []
                 if 1 <= s <= TILES * BLOCKS // 2:
                     for k in range(2):
                         t, j = divmod(2 * (s - 1) + k, BLOCKS)
-                        bk = bank(rolling())
+                        bk = bank(4 + 2 * (s % 2) + k)
                         nc.tensor.matmul(bk[:], lhsT=x_t[:, t * P:(t + 1) * P], rhs=wih_t[:, block_cols(j)], start=True, stop=True)
                         a_units.append((t, j, bk))
-                r_j, r_t = divmod(s - PASSES - 3, 2)
-                if r_j >= 0:
-                    r_bank = r_matmul(r_t, r_j, rolling())
+                if s >= STEPS - 1:
+                    for k in range(2):
+                        early_reads.append(first_round(len(early_reads), 4 + 2 * (s % 2) + k))
                 if s < STEPS:
-                    word_banks = transpose_words(h_stage if c < 0 else w_stage[c], q)
+                    word_banks = transpose_words(h_stage if c < 0 else w_stage[c], q, s)
                     grouped.append(grouped_tile())
                     if q == PASSES - 1 and len(w_stage) < BLOCKS:
                         load_w()
@@ -259,49 +262,59 @@ def tile_multilstm_pa_kernel(tc, x, h0, c0, w_ih1, w_hh1, lni_w1, lni_b1, lnh_w1
                         nc.sync.dma_start(out=c_rows[:], in_=c0.rearrange("(p t) h -> p t h", t=TILES))
                         nc.sync.dma_start(out=gain_c[:], in_=lnc_w1.partition_broadcast(P))
                         nc.sync.dma_start(out=bias_c[:], in_=lnc_b1.partition_broadcast(P))
-                if a_units:
-                    a_square(*a_units[0])
-                    a_gain(*a_units[1])
-                    a_gain(*a_units[0])
-                    a_square(*a_units[1])
-                if r_j >= 0:
-                    r_copy(r_t, r_j, r_bank)
+                if s == 0:
+                    mu_bank = bank(3)
+                    for t in range(TILES):
+                        nc.tensor.matmul(mu_bank[:, t:t + 1], lhsT=x_t32[:, t * P:(t + 1) * P], rhs=neg_wbar[:], start=True, stop=True)
+                    nc.vector.tensor_copy(out=neg_mu_a[:], in_=mu_bank[:, :TILES])
+                if s == 2:
+                    bias_bank = bank(3, BF16)
+                    nc.tensor.transpose(bias_bank[:, :P], vec_rows[:], ident_bf16[:])
+                copy_j, copy_t = divmod(s - PASSES - 4, 2)
+                if copy_j >= 0:
+                    r_copy(copy_t, copy_j, r_bank)
+                for unit in last_units:
+                    a_gain(*unit)
+                for unit in a_units:
+                    a_square(*unit)
+                if copy_j == 0:
+                    nc.scalar.activation(out=neg_shift[:, copy_t:copy_t + 1], in_=sums_r[:, 0, copy_t, 0:1], func=ACT.Copy,
+                                         scale=-1.0 / BANK)
+                if s == FIRST_RSTD_STEP:
+                    a_total = a_sum(0)
                 if s >= 1:
                     last_c, last_q = divmod(s - 1 - PASSES, PASSES)
                     codes = h_codes[:, last_q, :] if last_c < 0 else w_codes[:, last_c, last_q, :]
                     scales = h_scales[:, last_q, :] if last_c < 0 else w_scales[:, last_c, last_q, :]
                     nc.vector.quantize_mx(out=codes.bitcast(FP8X4), scales=scales, in_=grouped[s - 1][:])
-                if s >= PASSES + 4:
-                    r_square((s - PASSES - 4) % 2, (s - PASSES - 4) // 2)
-                if r_j == 0:
-                    nc.scalar.activation(out=neg_shift[:, r_t:r_t + 1], in_=sums_r[:, 0, r_t, 0:1], func=ACT.Copy, scale=-1.0 / BANK)
+                if s == FIRST_RSTD_STEP:
+                    a_rstd(a_total)
+                r_j, r_t = divmod(s - PASSES - 3, 2)
+                if r_j >= 0:
+                    r_bank = r_matmul(r_t, r_j, 3)
+                if s >= PASSES + 5:
+                    r_square((s - PASSES - 5) % 2, (s - PASSES - 5) // 2)
+                if s == STEPS:
+                    r_square(0, BLOCKS - 2)
+                if FIRST_RSTD_STEP < s <= FIRST_RSTD_STEP + 4:
+                    k = s - FIRST_RSTD_STEP - 1
+                    scale_u(k % 2, gate_cols((GATE_I, GATE_F)[k // 2]), "vector")
+                if s == 3:
+                    nc.scalar.copy(out=bias_i[:], in_=bias_bank[:, CHUNKS:2 * CHUNKS])
+                if s == 4:
+                    nc.vector.tensor_tensor(out=bias[:], in0=bias_bank[:, 2 * CHUNKS:3 * CHUNKS], in1=bias_i[:], op=ALU.add)
                 if s < STEPS:
                     interleave(grouped[s], 0, word_banks[0], SCALAR_COPIES[s] == 2)
                     interleave(grouped[s], 1, word_banks[1], SCALAR_COPIES[s] >= 1)
-                if s == 4:
-                    bias_bank = bank(rolling(), BF16)
-                    nc.tensor.transpose(bias_bank[:, :P], vec_rows[:], ident_bf16[:])
-                    nc.scalar.copy(out=bias_i[:], in_=bias_bank[:, CHUNKS:2 * CHUNKS])
-                    nc.vector.tensor_tensor(out=bias[:], in0=bias_bank[:, 2 * CHUNKS:3 * CHUNKS], in1=bias_i[:], op=ALU.add)
-                if s == FIRST_RSTD_STEP:
-                    a_rstd(0)
-                if FIRST_RSTD_STEP < s <= FIRST_RSTD_STEP + 8:
-                    k = s - FIRST_RSTD_STEP - 1
-                    scale_u(k % 2, gate_cols(k // 2), "vector")
-            a_rstd(1)
+            return r_bank
 
-        with tc.manual_schedule(engines={ENGINE.SP}):
-            stream_weights()
+        with tc.manual_schedule(engines={ENGINE.SP, ENGINE.PE, ENGINE.DVE, ENGINE.Activation, ENGINE.Pool}):
+            r_bank = stream_weights()
 
-        ctx.enter_context(tc.manual_schedule(engines={ENGINE.SP}))
+        ctx.enter_context(tc.manual_schedule())
         r_pair.append(shared.tile([P, 2, G], F32, name="r_second", tag="r_second", align_bytes=64, offset=0))
         neg_mu_r = small("neg_mu_r", 2)
         late = {}
-
-        def first_round(n, i):
-            j, tt = divmod(n, 2)
-            bk = r_matmul(2 + tt, j, i)
-            return lambda: nc.vector.bn_stats(out=bn_r[:, tt, j, :], in_=bk[:])
 
         def gate_block(pair, j, banks):
             gate = j // 2
@@ -331,12 +344,21 @@ def tile_multilstm_pa_kernel(tc, x, h0, c0, w_ih1, w_hh1, lni_w1, lni_b1, lnh_w1
             for t in range(2):
                 scale(r_cols(t, block_cols(j)), late["rstd_first"][:, t:t + 1], engine)
 
-        def second_round(j):
-            for tt in range(2):
-                nc.scalar.activation(out=r_cols(2 + tt, block_cols(j)), in_=r_matmul(2 + tt, j, 3 + tt)[:], func=ACT.Identity,
-                                     scale=late["rstd_second"][:, tt:tt + 1], bias=late["offset"][:, tt:tt + 1])
+        second_banks = {}
 
-        def gain_second(j):
+        def second_round(j, on_vector, banks=(3, 4)):
+            second_banks[j] = [r_matmul(2 + tt, j, banks[tt]) for tt in range(2)]
+            if not on_vector:
+                for tt in range(2):
+                    nc.scalar.activation(out=r_cols(2 + tt, block_cols(j)), in_=second_banks[j][tt][:], func=ACT.Identity,
+                                         scale=late["rstd_second"][:, tt:tt + 1], bias=late["offset"][:, tt:tt + 1])
+            else:
+                for tt in range(2):
+                    nc.vector.tensor_scalar(out=r_cols(2 + tt, block_cols(j)), in0=second_banks[j][tt][:],
+                                            scalar1=late["rstd_second"][:, tt:tt + 1], scalar2=late["offset"][:, tt:tt + 1],
+                                            op0=ALU.mult, op1=ALU.add)
+
+        def gain_second(j, on_vector):
             both = r_pair[1][:, :, block_cols(j)]
             nc.vector.tensor_tensor(out=both, in0=both, in1=gain_h[:, block_cols(j)].unsqueeze(1).to_broadcast([P, 2, BANK]),
                                     op=ALU.mult)
@@ -404,144 +426,150 @@ def tile_multilstm_pa_kernel(tc, x, h0, c0, w_ih1, w_hh1, lni_w1, lni_b1, lnh_w1
             nc.sync.dma_start(out=out_0.rearrange("(p t) h -> p t h", t=TILES)[:, t, :], in_=u[:, t, H:2 * H])
 
         last = BLOCKS - 1
-        r_last = [r_matmul(t, last, 4 + t) for t in range(2)]
-        reads = [first_round(n, (0, 1, 2, 3, 6, 7)[n]) for n in range(6)]
+        r_last = [r_matmul(t, last, t) for t in range(2)]
+        r_copy(1, last - 1, r_bank)
+        reads = early_reads + [first_round(4, 2), first_round(5, 3)]
         r_copy(0, last, r_last[0])
-        r_square(1, last - 1)
         r_copy(1, last, r_last[1])
+        r_square(1, last - 1)
         r_square(0, last)
         r_square(1, last)
-        for read in reads[:4]:
-            read()
-        total = small("r_total", 4)
-        nc.vector.tensor_reduce(out=total[:].rearrange("p (k t) -> p k t", k=2), in_=sums_r[:], axis=AXIS.X, op=ALU.add)
-        reads[4]()
-        nc.vector.tensor_scalar(out=neg_mu_r[:], in0=total[:, 0:2], scalar1=-1.0 / G, scalar2=None, op0=ALU.mult)
+        a_total = a_sum(1)
+        reads[0]()
+        a_rstd(a_total)
+        reads[1]()
+        reads[2]()
+        for t in range(2):
+            scale_u(t, gate_cols(GATE_G), "vector")
+        total = small("r_total", 2)
+        nc.vector.tensor_reduce(out=total[:], in_=sums_r[:, 0, :, :], axis=AXIS.X, op=ALU.add)
+        scale_u(0, gate_cols(GATE_O), "vector")
+        nc.vector.tensor_scalar(out=neg_mu_r[:], in0=total[:], scalar1=-1.0 / G, scalar2=None, op0=ALU.mult)
         parts = small("r_parts", 6)
-        nc.vector.scalar_tensor_tensor(out=parts[:, 0:2], in0=total[:, 0:2], scalar=1.0 / G, in1=neg_shift[:], op0=ALU.mult, op1=ALU.add)
-        nc.vector.scalar_tensor_tensor(out=parts[:, 2:4], in0=total[:, 0:2], scalar=-1.0 / G, in1=neg_shift[:], op0=ALU.mult,
+        nc.vector.scalar_tensor_tensor(out=parts[:, 0:2], in0=total[:], scalar=1.0 / G, in1=neg_shift[:], op0=ALU.mult, op1=ALU.add)
+        nc.vector.scalar_tensor_tensor(out=parts[:, 2:4], in0=total[:], scalar=-1.0 / G, in1=neg_shift[:], op0=ALU.mult,
                                        op1=ALU.subtract)
-        nc.vector.tensor_scalar(out=parts[:, 4:6], in0=total[:, 2:4], scalar1=1.0 / G, scalar2=EPS, op0=ALU.mult, op1=ALU.add)
+        scale_u(1, gate_cols(GATE_O), "vector")
         centre_first(0)
+        total = small("r_total", 2)
+        nc.vector.tensor_reduce(out=total[:], in_=sums_r[:, 1, :, :], axis=AXIS.X, op=ALU.add)
+        reads[3]()
+        nc.vector.tensor_scalar(out=parts[:, 4:6], in0=total[:], scalar1=1.0 / G, scalar2=EPS, op0=ALU.mult, op1=ALU.add)
         var = small("r_var", 2)
         for t in range(2):
             nc.vector.scalar_tensor_tensor(out=var[:, t:t + 1], in0=parts[:, t:t + 1], scalar=parts[:, 2 + t:3 + t],
                                            in1=parts[:, 4 + t:5 + t], op0=ALU.mult, op1=ALU.add)
         late["rstd_first"] = inverse_root(var[:], "r_rstd")
-        for t in (2, 3):
-            scale_u(t, gate_cols(GATE_I), "scalar")
+        for gate in (GATE_I, GATE_G)[:2]:
+            for t in (2, 3):
+                scale_u(t, gate_cols(gate), "scalar")
+        reads[4]()
         reads[5]()
-        reads = [first_round(6 + n, 3 + n) for n in range(2)]
-        reads[0]()
         scale_first(0, "vector")
-        reads[1]()
 
-        early = [2 * gate + half for gate in (GATE_I, GATE_G, GATE_F) for half in range(2)]
+        blocks = [2 * gate + half for gate in (GATE_I, GATE_G, GATE_F, GATE_O) for half in range(2)]
         turn = [0]
 
         def gate_banks():
             turn[0] += 2
             return (turn[0] % 3, (turn[0] + 1) % 3)
 
-        for n, j in enumerate(early):
-            if n + 1 < len(early):
-                centre_first(early[n + 1])
-            gate_block(0, j, gate_banks())
-            if n < 4:
-                reads = [first_round(8 + 2 * n + k, 3 + k) for k in range(2)]
-            if n + 1 < len(early):
-                scale_first(early[n + 1], "vector")
-            if n < 4:
-                for read in reads:
-                    read()
-            if n < 4:
-                scale_u(2 + n % 2, gate_cols((GATE_G, GATE_F)[n // 2]), "scalar")
-            if n == 3:
-                mean_var = small("r_mean_var", 4)
-                for tt in range(2):
-                    nc.vector.bn_aggr(out=mean_var[:, 2 * tt:2 * tt + 2], in_=bn_r[:, tt, :, :].rearrange("p j s -> p (j s)"))
-                c0_banks = [c0_transposed(t, 5 + t) for t in range(2)]
-            if n == 4:
-                var = small("r_var", 2)
-                nc.vector.tensor_scalar(out=var[:], in0=mean_var[:, 1::2], scalar1=EPS, scalar2=None, op0=ALU.add)
-                late["rstd_second"] = inverse_root(var[:], "r_rstd")
-                input_times_cell(0)
-                late["offset"] = small("r_offset", 2)
-                nc.vector.scalar_tensor_tensor(out=late["offset"][:], in0=mean_var[:, 0::2], scalar=-1.0, in1=late["rstd_second"][:],
-                                               op0=ALU.mult, op1=ALU.mult)
-                second_round(early[0])
-                input_times_cell(1)
-        second_round(early[1])
-        gain_second(early[0])
-        forget_times_c0(0, c0_banks[0])
-        forget_times_c0(1, c0_banks[1])
         cells = {}
         means = {}
         rstds = {}
-        for n, j in enumerate(early):
-            if n + 1 < len(early):
-                gain_second(early[n + 1])
-            gate_block(1, j, gate_banks())
-            if n + 2 < len(early):
-                second_round(early[n + 2])
-            if n == 0:
+        outs = {}
+        for n, j in enumerate(blocks):
+            if n < 5:
+                reads = [first_round(6 + 2 * n + k, 4 + (2 * n + k) % 4) for k in range(2)]
+            if n == 5:
+                c0_banks = [c0_transposed(t, 5 + t) for t in range(2)]
+                mean_var = small("r_mean_var", 4)
+                for tt in range(2):
+                    nc.vector.bn_aggr(out=mean_var[:, 2 * tt:2 * tt + 2], in_=bn_r[:, tt, :, :].rearrange("p j s -> p (j s)"))
+            if n + 1 < len(blocks):
+                centre_first(blocks[n + 1])
+            if n == 5:
+                var = small("r_var", 2)
+                nc.vector.tensor_scalar(out=var[:], in0=mean_var[:, 1::2], scalar1=EPS, scalar2=None, op0=ALU.add)
+                late["rstd_second"] = inverse_root(var[:], "r_rstd")
+            gate_block(0, j, gate_banks())
+            if n < 5:
+                reads[0]()
+            if n + 1 < len(blocks):
+                scale_first(blocks[n + 1], "vector" if n < 4 else "scalar")
+            if n < 5:
+                reads[1]()
+            if n < 4:
+                scale_u(2 + n % 2, gate_cols((GATE_F, GATE_O)[n // 2]), "scalar")
+            if n == 4:
+                input_times_cell(0)
+            if n == 5:
+                input_times_cell(1)
+                late["offset"] = small("r_offset", 2)
+                nc.vector.scalar_tensor_tensor(out=late["offset"][:], in0=mean_var[:, 0::2], scalar=-1.0, in1=late["rstd_second"][:],
+                                               op0=ALU.mult, op1=ALU.mult)
+                second_round(blocks[0], False)
+            if n == 6:
+                forget_times_c0(0, c0_banks[0])
+                second_round(blocks[1], False)
+                forget_times_c0(1, c0_banks[1])
                 cells[0] = back(0, (GATE_I, GATE_F), (7, 5))
-                centre_first(2 * GATE_O)
+                gain_second(blocks[0], False)
+            if n == 7:
                 parts = cell_parts(cells[0])
-                scale_first(2 * GATE_O, "vector")
+        for m, j in enumerate(blocks[:6]):
+            if m < 4:
+                second_round(blocks[m + 2], m + 2 in ())
+            if m < 5:
+                gain_second(blocks[m + 1], m + 1 in ())
+            gate_block(1, j, gate_banks())
+            if m == 0:
                 means[0] = cell_mean_var(parts)
-            if n == 1:
                 rstds[0] = cell_rstd(means[0])
                 cell_centre(0, cells[0], means[0])
                 cells[1] = back(1, (GATE_I, GATE_F), (6, 7))
+            if m == 1:
                 cell_finish(0, rstds[0])
-            if n == 2:
                 parts = cell_parts(cells[1])
-                centre_first(2 * GATE_O + 1)
+            if m == 2:
                 means[1] = cell_mean_var(parts)
-                scale_first(2 * GATE_O + 1, "vector")
-            if n == 3:
                 rstds[1] = cell_rstd(means[1])
                 cell_centre(1, cells[1], means[1])
-                cell_tanh(0)
-                for t in (2, 3):
-                    scale_u(t, gate_cols(GATE_O), "scalar")
-            if n == 4:
+            if m == 3:
                 c0_banks = [c0_transposed(t, 3 + t) for t in (2, 3)]
                 cell_finish(1, rstds[1])
+            if m == 4:
                 input_times_cell(2)
-            if n == 5:
                 input_times_cell(3)
-        gate_block(0, 2 * GATE_O, gate_banks())
-        second_round(2 * GATE_O)
+        second_round(blocks[6], False)
+        second_round(blocks[7], False, (7, 3))
         forget_times_c0(2, c0_banks[0])
         forget_times_c0(3, c0_banks[1])
-        gate_block(0, 2 * GATE_O + 1, gate_banks())
-        cells[2] = back(2, (GATE_I, GATE_F), (7, 5))
-        cell_tanh(1)
-        gain_second(2 * GATE_O)
-        second_round(2 * GATE_O + 1)
-        cells[3] = back(3, (GATE_I, GATE_F), (6, 0))
+        cell_tanh(0)
+        cells[2] = back(2, (GATE_I, GATE_F), (4, 5))
+        gain_second(blocks[6], False)
+        cells[3] = back(3, (GATE_I, GATE_F), (6, 7))
         parts = cell_parts(cells[2])
-        gain_second(2 * GATE_O + 1)
+        gate_block(1, blocks[6], (0, 1))
+        outs[0] = back(0, (GATE_O,), (3, 2))
+        gain_second(blocks[7], False)
         means[2] = cell_mean_var(parts)
-        gate_block(1, 2 * GATE_O, (1, 2))
+        cell_tanh(1)
         parts = cell_parts(cells[3])
         rstds[2] = cell_rstd(means[2])
-        outs0 = back(0, (GATE_O,), (3, 4))
+        gate_block(1, blocks[7], (0, 1))
         cell_centre(2, cells[2], means[2])
         means[3] = cell_mean_var(parts)
-        gate_block(1, 2 * GATE_O + 1, (1, 2))
-        cell_finish(2, rstds[2])
+        outs[1] = back(1, (GATE_O,), (4, 5))
+        hidden(0, outs[0])
         rstds[3] = cell_rstd(means[3])
-        cell_tanh(2)
         cell_centre(3, cells[3], means[3])
-        outs1 = back(1, (GATE_O,), (7, 5))
-        hidden(0, outs0)
+        cell_finish(2, rstds[2])
+        cell_tanh(2)
         cell_finish(3, rstds[3])
         cell_tanh(3)
-        outs2 = back(2, (GATE_O,), (3, 4))
-        outs3 = back(3, (GATE_O,), (6, 0))
-        hidden(1, outs1)
-        hidden(2, outs2)
-        hidden(3, outs3)
+        outs[2] = back(2, (GATE_O,), (3, 2))
+        outs[3] = back(3, (GATE_O,), (0, 1))
+        hidden(1, outs[1])
+        hidden(2, outs[2])
+        hidden(3, outs[3])

@@ -16,20 +16,23 @@ FP8X4 = mybir.dt.float8_e5m2_x4
 ACT = mybir.ActivationFunctionType
 ALU = mybir.AluOpType
 AXIS = mybir.AxisListType
-ENGINE = mybir.EngineType
 
 P = 128
 TILES = B // P
 BANK = 512
 BLOCKS = G // BANK
 CHUNKS = G // P
-PASSES = H // 512
+K_PASS = 4 * P
+PASSES = H // K_PASS
 GATE_I, GATE_F, GATE_G, GATE_O = 0, 1, 2, 3
 STAGE_BUFS = 3
 GROUPED_BUFS = 3
+SMALL_BUFS = 3
 STEPS = PASSES + BLOCKS * PASSES
-SCALAR_COPIES = (1, 1, 1, 1, 1, 0, 0, 1, 0, 1, 0, 1, 1, 0, 1, 1, 1, 1)
-FIRST_RSTD_STEP = 9
+A_STEPS = TILES * BLOCKS // 2
+FIRST_R_STEP = PASSES + 3
+A_RSTD_STEP = BLOCKS + 1
+CELL_BLOCKS = 6
 
 
 def tile_multilstm_pa_kernel(tc, x, h0, c0, w_ih1, w_hh1, lni_w1, lni_b1, lnh_w1, lnh_b1, lnc_w1, lnc_b1, out_0, out_1):
@@ -38,6 +41,7 @@ def tile_multilstm_pa_kernel(tc, x, h0, c0, w_ih1, w_hh1, lni_w1, lni_b1, lnh_w1
         keep = ctx.enter_context(tc.tile_pool(name="keep", bufs=1))
         shared = ctx.enter_context(tc.tile_pool(name="shared", bufs=1))
         psum = ctx.enter_context(tc.psum_pool(name="psum", bufs=1))
+        ctx.enter_context(tc.manual_schedule())
 
         def bank(i, dtype=F32):
             width = BANK if dtype == F32 else 2 * BANK
@@ -51,10 +55,10 @@ def tile_multilstm_pa_kernel(tc, x, h0, c0, w_ih1, w_hh1, lni_w1, lni_b1, lnh_w1
                                offset=STAGE_BUFS * 4 * H * 2)
 
         def small(name, width):
-            return keep.tile([P, width], F32, name=name, tag=name, bufs=3)
+            return keep.tile([P, width], F32, name=name, tag=name, bufs=SMALL_BUFS)
 
-        def discard():
-            return keep.tile([P, BANK], BF16, name="discard", tag="discard", bufs=3)
+        def squares_tile():
+            return keep.tile([P, BANK], BF16, name="squares", tag="squares", bufs=SMALL_BUFS)
 
         ident_f32 = keep.tile([P, P], F32, name="ident_f32")
         ident_bf16 = keep.tile([P, P], BF16, name="ident_bf16")
@@ -67,8 +71,8 @@ def tile_multilstm_pa_kernel(tc, x, h0, c0, w_ih1, w_hh1, lni_w1, lni_b1, lnh_w1
         x_t32 = keep.tile([P, B], F32, name="x_t32")
         wih_t = keep.tile([P, G], BF16, name="wih_t")
         wih_sums = keep.tile([P, 4], F32, name="wih_sums")
-        neg_wbar = keep.tile([P, 1], F32, name="neg_wbar")
-        neg_mu_a = keep.tile([P, TILES], F32, name="neg_mu_a")
+        neg_wih_mean = keep.tile([P, 1], F32, name="neg_wih_mean")
+        neg_mean_a = keep.tile([P, TILES], F32, name="neg_mean_a")
         gain_i = keep.tile([P, G], BF16, name="gain_i")
         gain_h = keep.tile([P, G], BF16, name="gain_h")
         gain_c = keep.tile([P, H], BF16, name="gain_c")
@@ -79,11 +83,12 @@ def tile_multilstm_pa_kernel(tc, x, h0, c0, w_ih1, w_hh1, lni_w1, lni_b1, lnh_w1
         w_codes = keep.tile([P, BLOCKS, PASSES, BANK], U32, name="w_codes", align_bytes=64)
         w_scales = keep.tile([P, BLOCKS, PASSES, BANK], U8, name="w_scales", align_bytes=64)
         u = keep.tile([P, TILES, G], F32, name="u")
-        ssq_a = keep.tile([P, TILES, BLOCKS], F32, name="ssq_a")
-        sums_r = keep.tile([P, 2, 2, BLOCKS], F32, name="sums_r")
+        v_pair = [keep.tile([P, 2, G], F32, name="v_first")]
+        squares_a = keep.tile([P, TILES, BLOCKS], F32, name="squares_a")
+        sums_r = keep.tile([P, 2, BLOCKS], F32, name="sums_r")
+        squares_r = keep.tile([P, 2, BLOCKS], F32, name="squares_r")
         neg_shift = keep.tile([P, 2], F32, name="neg_shift")
         bn_r = keep.tile([P, 2, BLOCKS, 6], F32, name="bn_r")
-        r_pair = [keep.tile([P, 2, G], F32, name="r_first")]
         rstd_a = []
 
         def block_cols(j):
@@ -92,13 +97,41 @@ def tile_multilstm_pa_kernel(tc, x, h0, c0, w_ih1, w_hh1, lni_w1, lni_b1, lnh_w1
         def gate_cols(gate):
             return slice(gate * H, (gate + 1) * H)
 
-        def r_cols(t, cols):
-            return r_pair[t // 2][:, t % 2, cols]
+        def v_cols(t, cols):
+            return v_pair[t // 2][:, t % 2, cols]
 
         def inverse_root(var, name):
             rstd = small(name, var.shape[1])
             nc.gpsimd.tensor_tensor(out=rstd[:], in0=var, in1=neg_half[:, :var.shape[1]], op=ALU.pow)
             return rstd
+
+        def scale(ap, factor, on_scalar):
+            if on_scalar:
+                nc.scalar.activation(out=ap, in_=ap, func=ACT.Copy, scale=factor)
+            else:
+                nc.vector.tensor_scalar(out=ap, in0=ap, scalar1=factor, scalar2=None, op0=ALU.mult)
+
+        def a_square(t, j, bk):
+            squares = squares_tile()
+            nc.scalar.activation(out=squares[:], in_=bk[:], func=ACT.Square, bias=neg_mean_a[:, t:t + 1],
+                                 accum_out=squares_a[:, t, j:j + 1])
+
+        def a_gain(t, j, bk):
+            nc.vector.scalar_tensor_tensor(out=u[:, t, block_cols(j)], in0=bk[:], scalar=neg_mean_a[:, t:t + 1],
+                                           in1=gain_i[:, block_cols(j)], op0=ALU.add, op1=ALU.mult)
+
+        def a_sum(pair):
+            total = small("a_total", 2)
+            nc.vector.tensor_reduce(out=total[:], in_=squares_a[:, 2 * pair:2 * pair + 2, :], axis=AXIS.X, op=ALU.add)
+            return total
+
+        def a_rstd(total):
+            var = small("a_var", 2)
+            nc.vector.tensor_scalar(out=var[:], in0=total[:], scalar1=1.0 / G, scalar2=EPS, op0=ALU.mult, op1=ALU.add)
+            rstd_a.append(inverse_root(var[:], "a_rstd"))
+
+        def scale_u(t, gate, on_scalar):
+            scale(u[:, t, gate_cols(gate)], rstd_a[t // 2][:, t % 2:t % 2 + 1], on_scalar)
 
         def r_matmul(t, j, i):
             bk = bank(i)
@@ -109,264 +142,220 @@ def tile_multilstm_pa_kernel(tc, x, h0, c0, w_ih1, w_hh1, lni_w1, lni_b1, lnh_w1
                                     start=(q == 0), stop=(q == PASSES - 1))
             return bk
 
-        def r_copy(t, j, bk):
-            nc.scalar.activation(out=r_cols(t, block_cols(j)), in_=bk[:], func=ACT.Copy, accum_out=sums_r[:, 0, t, j:j + 1])
+        def r_copy(n, bk):
+            j, t = divmod(n, 2)
+            nc.scalar.activation(out=v_cols(t, block_cols(j)), in_=bk[:], func=ACT.Copy, accum_out=sums_r[:, t, j:j + 1])
 
-        def r_square(t, j):
-            squares = discard()
-            nc.scalar.activation(out=squares[:], in_=r_cols(t, block_cols(j)), func=ACT.Square,
-                                 bias=neg_shift[:, t:t + 1], accum_out=sums_r[:, 1, t, j:j + 1])
-
-        def a_sum(pair):
-            total = small("a_total", 2)
-            nc.vector.tensor_reduce(out=total[:], in_=ssq_a[:, 2 * pair:2 * pair + 2, :], axis=AXIS.X, op=ALU.add)
-            return total
-
-        def a_rstd(total):
-            var = small("a_var", 2)
-            nc.vector.tensor_scalar(out=var[:], in0=total[:], scalar1=1.0 / G, scalar2=EPS, op0=ALU.mult, op1=ALU.add)
-            rstd_a.append(inverse_root(var[:], "a_rstd"))
-
-        def scale(ap, factor, engine):
-            if engine == "vector":
-                nc.vector.tensor_scalar(out=ap, in0=ap, scalar1=factor, scalar2=None, op0=ALU.mult)
-            elif engine == "gpsimd":
-                nc.gpsimd.tensor_scalar(out=ap, in0=ap, scalar1=factor, scalar2=0.0, op0=ALU.mult, op1=ALU.add)
-            else:
-                nc.scalar.activation(out=ap, in_=ap, func=ACT.Copy, scale=factor)
-
-        def scale_u(t, cols, engine):
-            scale(u[:, t, cols], rstd_a[t // 2][:, t % 2:t % 2 + 1], engine)
+        def r_square(n):
+            j, t = divmod(n, 2)
+            squares = squares_tile()
+            nc.scalar.activation(out=squares[:], in_=v_cols(t, block_cols(j)), func=ACT.Square,
+                                 bias=neg_shift[:, t:t + 1], accum_out=squares_r[:, t, j:j + 1])
 
         def first_round(n, i):
-            j, tt = divmod(n, 2)
-            bk = r_matmul(2 + tt, j, i)
-            return lambda: nc.vector.bn_stats(out=bn_r[:, tt, j, :], in_=bk[:])
+            j, t = divmod(n, 2)
+            bk = r_matmul(2 + t, j, i)
+            return lambda: nc.vector.bn_stats(out=bn_r[:, t, j, :], in_=bk[:])
 
-        early_reads = []
+        for k, vec in enumerate((lni_w1, lni_b1, lnh_b1)):
+            nc.sync.dma_start(out=vec_rows[k * CHUNKS:(k + 1) * CHUNKS, :], in_=vec.rearrange("(c p) -> c p", p=P))
+        nc.sync.dma_start(out=x_rows[:], in_=x.rearrange("(p t) v -> p t v", t=TILES))
+        wih_stage = stage_tile()
+        wih_rows = wih_stage[:].rearrange("p b (j c v) -> p (b j) c v", c=4, v=V)
+        for gate in range(4):
+            nc.sync.dma_start(out=wih_rows[:, 2 * gate:2 * (gate + 1), :, :],
+                              in_=w_ih1[gate_cols(gate), :].rearrange("(j p c) v -> p j c v", p=P, c=4))
+        h_stage = stage_tile()
+        nc.sync.dma_start(out=h_stage[:], in_=h0.rearrange("(p t) k -> p t k", t=TILES))
+        w_stage = []
 
-        def stream_weights():
-            for k, vec in enumerate((lni_w1, lni_b1, lnh_b1)):
-                nc.sync.dma_start(out=vec_rows[k * CHUNKS:(k + 1) * CHUNKS, :], in_=vec.rearrange("(c p) -> c p", p=P))
-            nc.sync.dma_start(out=x_rows[:], in_=x.rearrange("(p t) v -> p t v", t=TILES))
-            wih_stage = stage_tile()
-            wih_rows = wih_stage[:].rearrange("p b (j c v) -> p (b j) c v", c=4, v=V)
-            for k in range(4):
-                nc.sync.dma_start(out=wih_rows[:, 2 * k:2 * (k + 1), :, :],
-                                  in_=w_ih1[gate_cols(k), :].rearrange("(j p c) v -> p j c v", p=P, c=4))
-            h_stage = stage_tile()
-            nc.sync.dma_start(out=h_stage[:], in_=h0.rearrange("(p t) k -> p t k", t=TILES))
-            w_stage = []
+        def load_w():
+            rows = w_hh1[block_cols(len(w_stage)), :]
+            w_stage.append(stage_tile())
+            nc.sync.dma_start(out=w_stage[-1][:], in_=rows.rearrange("(b p) k -> p b k", p=P))
 
-            def load_w():
-                rows = w_hh1[block_cols(len(w_stage)), :]
-                w_stage.append(stage_tile())
-                nc.sync.dma_start(out=w_stage[-1][:], in_=rows.rearrange("(b p) k -> p b k", p=P))
+        load_w()
+        nc.gpsimd.memset(vec_rows[3 * CHUNKS:, :], 0.0)
+        make_identity(nc, ident_bf16[:])
+        make_identity(nc, ident_f32[:])
+        nc.gpsimd.memset(neg_half[:], -0.5)
 
-            load_w()
-            nc.gpsimd.memset(vec_rows[3 * CHUNKS:, :], 0.0)
-            make_identity(nc, ident_bf16[:])
-            make_identity(nc, ident_f32[:])
-            nc.gpsimd.memset(neg_half[:], -0.5)
+        def spread_gain(gate, i):
+            bk = bank(i, BF16)
+            for c in range(H // P):
+                row = gate * (H // P) + c
+                nc.tensor.matmul(bk[:, c * P:(c + 1) * P], lhsT=ident_bf16[:, row:row + 1].to_broadcast([P, P]),
+                                 rhs=vec_rows[:], start=True, stop=True)
+            if gate == GATE_O:
+                nc.vector.tensor_copy(out=gain_i[:, gate_cols(gate)], in_=bk[:])
+            else:
+                nc.scalar.copy(out=gain_i[:, gate_cols(gate)], in_=bk[:])
 
-            def spread_gain(k, i):
-                bk = bank(i, BF16)
-                for c in range(8):
-                    nc.tensor.matmul(bk[:, c * P:(c + 1) * P], lhsT=ident_bf16[:, 8 * k + c:8 * k + c + 1].to_broadcast([P, P]),
-                                     rhs=vec_rows[:], start=True, stop=True)
-                if k < 3:
-                    nc.scalar.copy(out=gain_i[:, gate_cols(k)], in_=bk[:])
-                else:
-                    nc.vector.tensor_copy(out=gain_i[:, gate_cols(k)], in_=bk[:])
+        def transpose_wih(gate, i):
+            bk = bank(i, BF16)
+            for jc in range(H // P):
+                nc.tensor.transpose(bk[:, jc * P:(jc + 1) * P], wih_rows[:, 2 * gate + jc // 4, jc % 4, :], ident_bf16[:])
+            dst = wih_t[:, gate_cols(gate)].rearrange("p (j r c) -> p j r c", j=2, c=4)
+            src = bk[:].rearrange("p (j c r) -> p j r c", j=2, c=4)
+            if gate % 2 == 0:
+                nc.scalar.activation(out=dst, in_=src, func=ACT.Copy, accum_out=wih_sums[:, gate:gate + 1])
+            else:
+                nc.vector.tensor_scalar(out=dst, in0=src, scalar1=1.0, scalar2=None, op0=ALU.mult, op1=ALU.add,
+                                        accum_out=wih_sums[:, gate:gate + 1])
 
-            def transpose_wih(k, i):
-                bk = bank(i, BF16)
-                for jc in range(8):
-                    nc.tensor.transpose(bk[:, jc * P:(jc + 1) * P], wih_rows[:, 2 * k + jc // 4, jc % 4, :], ident_bf16[:])
-                dst = wih_t[:, gate_cols(k)].rearrange("p (j r c) -> p j r c", j=2, c=4)
-                src = bk[:].rearrange("p (j c r) -> p j r c", j=2, c=4)
-                if k % 2 == 0:
-                    nc.scalar.activation(out=dst, in_=src, func=ACT.Copy, accum_out=wih_sums[:, k:k + 1])
-                else:
-                    nc.vector.tensor_scalar(out=dst, in0=src, scalar1=1.0, scalar2=None, op0=ALU.mult, op1=ALU.add,
-                                            accum_out=wih_sums[:, k:k + 1])
+        spread_gain(GATE_I, 5)
+        spread_gain(GATE_F, 6)
+        x_bank = bank(0, BF16)
+        for t in range(TILES):
+            nc.tensor.transpose(x_bank[:, t * P:(t + 1) * P], x_rows[:, t, :], ident_bf16[:])
+        nc.vector.tensor_copy(out=x_t[:], in_=x_bank[:, :B])
+        nc.vector.tensor_copy(out=x_t32[:], in_=x_bank[:, :B])
+        for gate in range(4):
+            transpose_wih(gate, 1 + gate)
+        scaled_sums = small("scaled_sums", 4)
+        nc.vector.tensor_scalar(out=scaled_sums[:], in0=wih_sums[:], scalar1=-1.0 / G, scalar2=None, op0=ALU.mult, op1=ALU.add,
+                                accum_out=neg_wih_mean[:])
+        load_w()
+        spread_gain(GATE_G, 5)
+        spread_gain(GATE_O, 6)
 
-            spread_gain(0, 5)
-            spread_gain(1, 6)
-            x_bank = bank(0, BF16)
-            for t in range(TILES):
-                nc.tensor.transpose(x_bank[:, t * P:(t + 1) * P], x_rows[:, t, :], ident_bf16[:])
-            nc.vector.tensor_copy(out=x_t[:], in_=x_bank[:, :B])
-            nc.vector.tensor_copy(out=x_t32[:], in_=x_bank[:, :B])
-
-            for k in range(4):
-                transpose_wih(k, 1 + k)
-            scaled_sums = small("scaled_sums", 4)
-            nc.vector.tensor_scalar(out=scaled_sums[:], in0=wih_sums[:], scalar1=-1.0 / G, scalar2=None, op0=ALU.mult, op1=ALU.add,
-                                    accum_out=neg_wbar[:])
-            load_w()
-            spread_gain(2, 5)
-            spread_gain(3, 6)
-
-            def transpose_words(stage, q, s):
-                banks = []
-                for half in range(2):
-                    bk = bank((2 * s + half) % 3)
-                    view = bk[:].rearrange("p (b w r) -> p b w r", b=2, w=2)
-                    for b in range(2):
-                        words = stage[:, 2 * half + b, :].bitcast(F32)
-                        for w in range(2):
-                            nc.tensor.transpose(view[:, b, w, :], words[:, 256 * q + w:256 * (q + 1):2], ident_f32[:])
-                    banks.append(bk)
-                return banks
-
-            def interleave(grouped, half, bk, on_scalar):
-                dst = grouped[:].bitcast(F32)[:, block_cols(half)].rearrange("p (b r w) -> p b r w", b=2, w=2)
-                src = bk[:].rearrange("p (b w r) -> p b r w", b=2, w=2)
-                if on_scalar:
-                    nc.scalar.copy(out=dst, in_=src)
-                else:
-                    nc.vector.tensor_copy(out=dst, in_=src)
-
-            def a_square(t, j, bk):
-                squares = discard()
-                nc.scalar.activation(out=squares[:], in_=bk[:], func=ACT.Square, bias=neg_mu_a[:, t:t + 1],
-                                     accum_out=ssq_a[:, t, j:j + 1])
-
-            def a_gain(t, j, bk):
-                nc.vector.scalar_tensor_tensor(out=u[:, t, block_cols(j)], in0=bk[:], scalar=neg_mu_a[:, t:t + 1],
-                                               in1=gain_i[:, block_cols(j)], op0=ALU.add, op1=ALU.mult)
-
-            grouped = []
-            a_units = []
-            for s in range(STEPS + 1):
-                c, q = divmod(s - PASSES, PASSES)
-                last_units = a_units
-                a_units = []
-                if 1 <= s <= TILES * BLOCKS // 2:
-                    for k in range(2):
-                        t, j = divmod(2 * (s - 1) + k, BLOCKS)
-                        bk = bank(4 + 2 * (s % 2) + k)
-                        nc.tensor.matmul(bk[:], lhsT=x_t[:, t * P:(t + 1) * P], rhs=wih_t[:, block_cols(j)], start=True, stop=True)
-                        a_units.append((t, j, bk))
-                if s >= STEPS - 1:
-                    for k in range(2):
-                        early_reads.append(first_round(len(early_reads), 4 + 2 * (s % 2) + k))
-                if s < STEPS:
-                    word_banks = transpose_words(h_stage if c < 0 else w_stage[c], q, s)
-                    grouped.append(grouped_tile())
-                    if q == PASSES - 1 and len(w_stage) < BLOCKS:
-                        load_w()
-                    if q == PASSES - 1 and c + STAGE_BUFS == BLOCKS:
-                        nc.sync.dma_start(out=gain_h[:], in_=lnh_w1.partition_broadcast(P))
-                        nc.sync.dma_start(out=c_rows[:], in_=c0.rearrange("(p t) h -> p t h", t=TILES))
-                        nc.sync.dma_start(out=gain_c[:], in_=lnc_w1.partition_broadcast(P))
-                        nc.sync.dma_start(out=bias_c[:], in_=lnc_b1.partition_broadcast(P))
-                if s == 0:
-                    mu_bank = bank(3)
-                    for t in range(TILES):
-                        nc.tensor.matmul(mu_bank[:, t:t + 1], lhsT=x_t32[:, t * P:(t + 1) * P], rhs=neg_wbar[:], start=True, stop=True)
-                    nc.vector.tensor_copy(out=neg_mu_a[:], in_=mu_bank[:, :TILES])
-                if s == 2:
-                    bias_bank = bank(3, BF16)
-                    nc.tensor.transpose(bias_bank[:, :P], vec_rows[:], ident_bf16[:])
-                copy_j, copy_t = divmod(s - PASSES - 4, 2)
-                if copy_j >= 0:
-                    r_copy(copy_t, copy_j, r_bank)
-                for unit in last_units:
-                    a_gain(*unit)
-                for unit in a_units:
-                    a_square(*unit)
-                if copy_j == 0:
-                    nc.scalar.activation(out=neg_shift[:, copy_t:copy_t + 1], in_=sums_r[:, 0, copy_t, 0:1], func=ACT.Copy,
-                                         scale=-1.0 / BANK)
-                if s == FIRST_RSTD_STEP:
-                    a_total = a_sum(0)
-                if s >= 1:
-                    last_c, last_q = divmod(s - 1 - PASSES, PASSES)
-                    codes = h_codes[:, last_q, :] if last_c < 0 else w_codes[:, last_c, last_q, :]
-                    scales = h_scales[:, last_q, :] if last_c < 0 else w_scales[:, last_c, last_q, :]
-                    nc.vector.quantize_mx(out=codes.bitcast(FP8X4), scales=scales, in_=grouped[s - 1][:])
-                if s == FIRST_RSTD_STEP:
-                    a_rstd(a_total)
-                r_j, r_t = divmod(s - PASSES - 3, 2)
-                if r_j >= 0:
-                    r_bank = r_matmul(r_t, r_j, 3)
-                if s >= PASSES + 5:
-                    r_square((s - PASSES - 5) % 2, (s - PASSES - 5) // 2)
-                if s == STEPS:
-                    r_square(0, BLOCKS - 2)
-                if FIRST_RSTD_STEP < s <= FIRST_RSTD_STEP + 4:
-                    k = s - FIRST_RSTD_STEP - 1
-                    scale_u(k % 2, gate_cols((GATE_I, GATE_F)[k // 2]), "vector")
-                if s == 3:
-                    nc.scalar.copy(out=bias_i[:], in_=bias_bank[:, CHUNKS:2 * CHUNKS])
-                if s == 4:
-                    nc.vector.tensor_tensor(out=bias[:], in0=bias_bank[:, 2 * CHUNKS:3 * CHUNKS], in1=bias_i[:], op=ALU.add)
-                if s < STEPS:
-                    interleave(grouped[s], 0, word_banks[0], SCALAR_COPIES[s] == 2)
-                    interleave(grouped[s], 1, word_banks[1], SCALAR_COPIES[s] >= 1)
-            return r_bank
-
-        with tc.manual_schedule(engines={ENGINE.SP, ENGINE.PE, ENGINE.DVE, ENGINE.Activation, ENGINE.Pool}):
-            r_bank = stream_weights()
-
-        ctx.enter_context(tc.manual_schedule())
-        r_pair.append(shared.tile([P, 2, G], F32, name="r_second", tag="r_second", align_bytes=64, offset=0))
-        neg_mu_r = small("neg_mu_r", 2)
-        late = {}
-
-        def gate_block(pair, j, banks):
-            gate = j // 2
+        def transpose_words(stage, q, s):
+            banks = []
             for half in range(2):
-                bk = bank(banks[half])
-                view = bk[:].rearrange("p (c t b) -> p c t b", c=2, t=2)
-                chunks = [4 * j + 2 * half + cc for cc in range(2)]
-                for cc, chunk in enumerate(chunks):
-                    cols = slice(chunk * P, (chunk + 1) * P)
-                    for tt in range(2):
-                        t = 2 * pair + tt
-                        nc.tensor.matmul(view[:, cc, tt, :], lhsT=u[:, t, cols], rhs=ident_f32[:], start=True, stop=False,
-                                         is_transpose=True)
-                        nc.tensor.matmul(view[:, cc, tt, :], lhsT=r_cols(t, cols), rhs=ident_f32[:], start=False, stop=True,
-                                         is_transpose=True)
-                for cc, chunk in enumerate(chunks):
-                    nc.scalar.activation(out=r_pair[pair][:, :, chunk * P:(chunk + 1) * P], in_=view[:, cc, :, :],
-                                         func=ACT.Tanh if gate == GATE_G else ACT.Sigmoid, bias=bias[:, chunk:chunk + 1])
+                bk = bank((2 * s + half) % 3)
+                view = bk[:].rearrange("p (b w r) -> p b w r", b=2, w=2)
+                for b in range(2):
+                    words = stage[:, 2 * half + b, :].bitcast(F32)
+                    for w in range(2):
+                        nc.tensor.transpose(view[:, b, w, :], words[:, q * K_PASS // 2 + w:(q + 1) * K_PASS // 2:2], ident_f32[:])
+                banks.append(bk)
+            return banks
 
-        def centre_first(j):
+        def interleave(grouped, half, bk, on_scalar):
+            dst = grouped[:].bitcast(F32)[:, block_cols(half)].rearrange("p (b r w) -> p b r w", b=2, w=2)
+            src = bk[:].rearrange("p (b w r) -> p b r w", b=2, w=2)
+            if on_scalar:
+                nc.scalar.copy(out=dst, in_=src)
+            else:
+                nc.vector.tensor_copy(out=dst, in_=src)
+
+        grouped = []
+        a_units = []
+        reads = []
+        early_scalings = [(t, gate) for gate in (GATE_I, GATE_F) for t in range(2)]
+        for s in range(STEPS + 1):
+            w_block, q = divmod(s - PASSES, PASSES)
+            last_a_units = a_units
+            a_units = []
+            if 1 <= s <= A_STEPS:
+                for k in range(2):
+                    t, j = divmod(2 * (s - 1) + k, BLOCKS)
+                    bk = bank(4 + 2 * (s % 2) + k)
+                    nc.tensor.matmul(bk[:], lhsT=x_t[:, t * P:(t + 1) * P], rhs=wih_t[:, block_cols(j)], start=True, stop=True)
+                    a_units.append((t, j, bk))
+            if s > A_STEPS:
+                for k in range(2):
+                    reads.append(first_round(len(reads), 4 + 2 * (s % 2) + k))
+            if s < STEPS:
+                word_banks = transpose_words(h_stage if w_block < 0 else w_stage[w_block], q, s)
+                grouped.append(grouped_tile())
+                if q == PASSES - 1 and len(w_stage) < BLOCKS:
+                    load_w()
+                if q == PASSES - 1 and w_block + STAGE_BUFS == BLOCKS:
+                    nc.sync.dma_start(out=gain_h[:], in_=lnh_w1.partition_broadcast(P))
+                    nc.sync.dma_start(out=c_rows[:], in_=c0.rearrange("(p t) h -> p t h", t=TILES))
+                    nc.sync.dma_start(out=gain_c[:], in_=lnc_w1.partition_broadcast(P))
+                    nc.sync.dma_start(out=bias_c[:], in_=lnc_b1.partition_broadcast(P))
+            if s == 0:
+                mean_bank = bank(3)
+                for t in range(TILES):
+                    nc.tensor.matmul(mean_bank[:, t:t + 1], lhsT=x_t32[:, t * P:(t + 1) * P], rhs=neg_wih_mean[:], start=True, stop=True)
+                nc.vector.tensor_copy(out=neg_mean_a[:], in_=mean_bank[:, :TILES])
+            if s == FIRST_R_STEP - 3:
+                bias_bank = bank(3, BF16)
+                nc.tensor.transpose(bias_bank[:, :P], vec_rows[:], ident_bf16[:])
+            unit = s - FIRST_R_STEP
+            if unit >= 1:
+                r_copy(unit - 1, r_bank)
+            for a_unit in last_a_units:
+                a_gain(*a_unit)
+            for a_unit in a_units:
+                a_square(*a_unit)
+            if unit in (1, 2):
+                nc.scalar.activation(out=neg_shift[:, unit - 1:unit], in_=sums_r[:, unit - 1, 0:1], func=ACT.Copy, scale=-1.0 / BANK)
+            if s in (A_RSTD_STEP, STEPS):
+                a_total = a_sum(len(rstd_a))
+            if s == STEPS:
+                reads[0]()
+            if s >= 1:
+                last_block, last_q = divmod(s - 1 - PASSES, PASSES)
+                codes = h_codes[:, last_q, :] if last_block < 0 else w_codes[:, last_block, last_q, :]
+                scales = h_scales[:, last_q, :] if last_block < 0 else w_scales[:, last_block, last_q, :]
+                nc.vector.quantize_mx(out=codes.bitcast(FP8X4), scales=scales, in_=grouped[s - 1][:])
+            if s in (A_RSTD_STEP, STEPS):
+                a_rstd(a_total)
+            if unit >= 0:
+                r_bank = r_matmul(unit % 2, unit // 2, 3)
+            if unit >= 2:
+                r_square(unit - 2)
+            if s == STEPS:
+                r_square(unit - 1)
+            scales_u = s > A_RSTD_STEP and len(early_scalings) > 0
+            if scales_u:
+                scale_u(*early_scalings.pop(0), False)
+            if s == FIRST_R_STEP - 2:
+                nc.scalar.copy(out=bias_i[:], in_=bias_bank[:, CHUNKS:2 * CHUNKS])
+            if s == FIRST_R_STEP - 1:
+                nc.vector.tensor_tensor(out=bias[:], in0=bias_bank[:, 2 * CHUNKS:3 * CHUNKS], in1=bias_i[:], op=ALU.add)
+            if s < STEPS:
+                scalar_takes_both = s in range(2, FIRST_R_STEP, 2)
+                vector_takes_both = FIRST_R_STEP <= s <= A_STEPS and not scales_u and s % 3 != 1
+                interleave(grouped[s], 0, word_banks[0], scalar_takes_both)
+                interleave(grouped[s], 1, word_banks[1], not vector_takes_both)
+
+        v_pair.append(shared.tile([P, 2, G], F32, name="v_second", tag="v_second", align_bytes=64, offset=0))
+
+        def centre_first(j, neg_mean):
             for t in range(2):
-                ap = r_cols(t, block_cols(j))
-                nc.vector.scalar_tensor_tensor(out=ap, in0=ap, scalar=neg_mu_r[:, t:t + 1], in1=gain_h[:, block_cols(j)],
+                ap = v_cols(t, block_cols(j))
+                nc.vector.scalar_tensor_tensor(out=ap, in0=ap, scalar=neg_mean[:, t:t + 1], in1=gain_h[:, block_cols(j)],
                                                op0=ALU.add, op1=ALU.mult)
 
-        def scale_first(j, engine):
+        def scale_first(j, rstd, on_scalar):
             for t in range(2):
-                scale(r_cols(t, block_cols(j)), late["rstd_first"][:, t:t + 1], engine)
+                scale(v_cols(t, block_cols(j)), rstd[:, t:t + 1], on_scalar)
 
-        second_banks = {}
+        def second_round(j, rstd, offset, banks=(3, 4)):
+            tiles = [r_matmul(2 + t, j, banks[t]) for t in range(2)]
+            for t in range(2):
+                nc.scalar.activation(out=v_cols(2 + t, block_cols(j)), in_=tiles[t][:], func=ACT.Identity,
+                                     scale=rstd[:, t:t + 1], bias=offset[:, t:t + 1])
 
-        def second_round(j, on_vector, banks=(3, 4)):
-            second_banks[j] = [r_matmul(2 + tt, j, banks[tt]) for tt in range(2)]
-            if not on_vector:
-                for tt in range(2):
-                    nc.scalar.activation(out=r_cols(2 + tt, block_cols(j)), in_=second_banks[j][tt][:], func=ACT.Identity,
-                                         scale=late["rstd_second"][:, tt:tt + 1], bias=late["offset"][:, tt:tt + 1])
-            else:
-                for tt in range(2):
-                    nc.vector.tensor_scalar(out=r_cols(2 + tt, block_cols(j)), in0=second_banks[j][tt][:],
-                                            scalar1=late["rstd_second"][:, tt:tt + 1], scalar2=late["offset"][:, tt:tt + 1],
-                                            op0=ALU.mult, op1=ALU.add)
-
-        def gain_second(j, on_vector):
-            both = r_pair[1][:, :, block_cols(j)]
+        def gain_second(j):
+            both = v_pair[1][:, :, block_cols(j)]
             nc.vector.tensor_tensor(out=both, in0=both, in1=gain_h[:, block_cols(j)].unsqueeze(1).to_broadcast([P, 2, BANK]),
                                     op=ALU.mult)
 
-        def input_times_cell(t, engine="vector"):
-            ap = r_cols(t, gate_cols(GATE_I))
-            eng = nc.vector if engine == "vector" else nc.gpsimd
-            eng.tensor_tensor(out=ap, in0=ap, in1=r_cols(t, gate_cols(GATE_G)), op=ALU.mult)
+        def transpose_sum(out, terms):
+            for k, term in enumerate(terms):
+                nc.tensor.matmul(out, lhsT=term, rhs=ident_f32[:], start=(k == 0), stop=(k == len(terms) - 1), is_transpose=True)
+
+        def gate_block(pair, j, banks):
+            for half in range(2):
+                bk = bank(banks[half])
+                view = bk[:].rearrange("p (c t b) -> p c t b", c=2, t=2)
+                chunks = [4 * j + 2 * half + c for c in range(2)]
+                for c, chunk in enumerate(chunks):
+                    cols = slice(chunk * P, (chunk + 1) * P)
+                    for t in range(2):
+                        transpose_sum(view[:, c, t, :], [u[:, 2 * pair + t, cols], v_cols(2 * pair + t, cols)])
+                for c, chunk in enumerate(chunks):
+                    nc.scalar.activation(out=v_pair[pair][:, :, chunk * P:(chunk + 1) * P], in_=view[:, c, :, :],
+                                         func=ACT.Tanh if j // 2 == GATE_G else ACT.Sigmoid, bias=bias[:, chunk:chunk + 1])
+
+        def input_times_cell(t):
+            ap = v_cols(t, gate_cols(GATE_I))
+            nc.vector.tensor_tensor(out=ap, in0=ap, in1=v_cols(t, gate_cols(GATE_G)), op=ALU.mult)
 
         def c0_transposed(t, i):
             bk = bank(i, BF16)
@@ -375,18 +364,16 @@ def tile_multilstm_pa_kernel(tc, x, h0, c0, w_ih1, w_hh1, lni_w1, lni_b1, lnh_w1
             return bk
 
         def forget_times_c0(t, bk):
-            ap = r_cols(t, gate_cols(GATE_F))
+            ap = v_cols(t, gate_cols(GATE_F))
             nc.vector.tensor_tensor(out=ap, in0=bk[:], in1=ap, op=ALU.mult)
 
-        def back(t, gates, banks):
+        def to_rows(t, gates, banks):
             tiles = []
             for half in range(2):
                 bk = bank(banks[half])
-                for jj in range(4):
-                    first = (4 * half + jj) * P
-                    for k, gate in enumerate(gates):
-                        nc.tensor.matmul(bk[:, jj * P:(jj + 1) * P], lhsT=r_cols(t, slice(gate * H + first, gate * H + first + P)),
-                                         rhs=ident_f32[:], start=(k == 0), stop=(k == len(gates) - 1), is_transpose=True)
+                for c in range(BANK // P):
+                    first = half * BANK + c * P
+                    transpose_sum(bk[:, c * P:(c + 1) * P], [v_cols(t, slice(gate * H + first, gate * H + first + P)) for gate in gates])
                 tiles.append(bk)
             return tiles
 
@@ -425,151 +412,146 @@ def tile_multilstm_pa_kernel(tc, x, h0, c0, w_ih1, w_hh1, lni_w1, lni_b1, lnh_w1
                 nc.vector.tensor_tensor(out=ap, in0=tiles[half][:], in1=ap, op=ALU.mult)
             nc.sync.dma_start(out=out_0.rearrange("(p t) h -> p t h", t=TILES)[:, t, :], in_=u[:, t, H:2 * H])
 
-        last = BLOCKS - 1
-        r_last = [r_matmul(t, last, t) for t in range(2)]
-        r_copy(1, last - 1, r_bank)
-        reads = early_reads + [first_round(4, 2), first_round(5, 3)]
-        r_copy(0, last, r_last[0])
-        r_copy(1, last, r_last[1])
-        r_square(1, last - 1)
-        r_square(0, last)
-        r_square(1, last)
-        a_total = a_sum(1)
-        reads[0]()
-        a_rstd(a_total)
+        last_units = [2 * BLOCKS - 2, 2 * BLOCKS - 1]
+        last_banks = [r_matmul(n % 2, n // 2, n % 2) for n in last_units]
+        r_copy(unit, r_bank)
+        reads.extend([first_round(4, 2), first_round(5, 3)])
+        for n, bk in zip(last_units, last_banks):
+            r_copy(n, bk)
+        for n in [unit] + last_units:
+            r_square(n)
         reads[1]()
         reads[2]()
         for t in range(2):
-            scale_u(t, gate_cols(GATE_G), "vector")
+            scale_u(t, GATE_G, False)
         total = small("r_total", 2)
-        nc.vector.tensor_reduce(out=total[:], in_=sums_r[:, 0, :, :], axis=AXIS.X, op=ALU.add)
-        scale_u(0, gate_cols(GATE_O), "vector")
-        nc.vector.tensor_scalar(out=neg_mu_r[:], in0=total[:], scalar1=-1.0 / G, scalar2=None, op0=ALU.mult)
-        parts = small("r_parts", 6)
-        nc.vector.scalar_tensor_tensor(out=parts[:, 0:2], in0=total[:], scalar=1.0 / G, in1=neg_shift[:], op0=ALU.mult, op1=ALU.add)
-        nc.vector.scalar_tensor_tensor(out=parts[:, 2:4], in0=total[:], scalar=-1.0 / G, in1=neg_shift[:], op0=ALU.mult,
+        nc.vector.tensor_reduce(out=total[:], in_=sums_r[:], axis=AXIS.X, op=ALU.add)
+        scale_u(0, GATE_O, False)
+        neg_mean_r = small("r_neg_mean", 2)
+        nc.vector.tensor_scalar(out=neg_mean_r[:], in0=total[:], scalar1=-1.0 / G, scalar2=None, op0=ALU.mult)
+        terms = small("r_terms", 6)
+        nc.vector.scalar_tensor_tensor(out=terms[:, 0:2], in0=total[:], scalar=1.0 / G, in1=neg_shift[:], op0=ALU.mult, op1=ALU.add)
+        nc.vector.scalar_tensor_tensor(out=terms[:, 2:4], in0=total[:], scalar=-1.0 / G, in1=neg_shift[:], op0=ALU.mult,
                                        op1=ALU.subtract)
-        scale_u(1, gate_cols(GATE_O), "vector")
-        centre_first(0)
+        scale_u(1, GATE_O, False)
+        blocks = [2 * gate + half for gate in (GATE_I, GATE_G, GATE_F, GATE_O) for half in range(2)]
+        centre_first(blocks[0], neg_mean_r)
         total = small("r_total", 2)
-        nc.vector.tensor_reduce(out=total[:], in_=sums_r[:, 1, :, :], axis=AXIS.X, op=ALU.add)
+        nc.vector.tensor_reduce(out=total[:], in_=squares_r[:], axis=AXIS.X, op=ALU.add)
         reads[3]()
-        nc.vector.tensor_scalar(out=parts[:, 4:6], in0=total[:], scalar1=1.0 / G, scalar2=EPS, op0=ALU.mult, op1=ALU.add)
+        nc.vector.tensor_scalar(out=terms[:, 4:6], in0=total[:], scalar1=1.0 / G, scalar2=EPS, op0=ALU.mult, op1=ALU.add)
         var = small("r_var", 2)
         for t in range(2):
-            nc.vector.scalar_tensor_tensor(out=var[:, t:t + 1], in0=parts[:, t:t + 1], scalar=parts[:, 2 + t:3 + t],
-                                           in1=parts[:, 4 + t:5 + t], op0=ALU.mult, op1=ALU.add)
-        late["rstd_first"] = inverse_root(var[:], "r_rstd")
-        for gate in (GATE_I, GATE_G)[:2]:
+            nc.vector.scalar_tensor_tensor(out=var[:, t:t + 1], in0=terms[:, t:t + 1], scalar=terms[:, 2 + t:3 + t],
+                                           in1=terms[:, 4 + t:5 + t], op0=ALU.mult, op1=ALU.add)
+        rstd_first = inverse_root(var[:], "r_rstd")
+        for gate in (GATE_I, GATE_G):
             for t in (2, 3):
-                scale_u(t, gate_cols(gate), "scalar")
+                scale_u(t, gate, True)
         reads[4]()
         reads[5]()
-        scale_first(0, "vector")
+        scale_first(blocks[0], rstd_first, False)
 
-        blocks = [2 * gate + half for gate in (GATE_I, GATE_G, GATE_F, GATE_O) for half in range(2)]
-        turn = [0]
+        turns = [0]
 
         def gate_banks():
-            turn[0] += 2
-            return (turn[0] % 3, (turn[0] + 1) % 3)
+            turns[0] += 1
+            return (2 * turns[0] % 3, (2 * turns[0] + 1) % 3)
 
-        cells = {}
-        means = {}
-        rstds = {}
-        outs = {}
+        first_round_turns = (2 * BLOCKS - len(reads)) // 2
+        stats_turn = first_round_turns
+        late_scalings = [(t, gate) for gate in (GATE_F, GATE_O) for t in (2, 3)]
         for n, j in enumerate(blocks):
-            if n < 5:
-                reads = [first_round(6 + 2 * n + k, 4 + (2 * n + k) % 4) for k in range(2)]
-            if n == 5:
+            if n < first_round_turns:
+                reads.extend([first_round(len(reads) + k, 4 + (2 * n + k) % 4) for k in range(2)])
+            if n == stats_turn:
                 c0_banks = [c0_transposed(t, 5 + t) for t in range(2)]
-                mean_var = small("r_mean_var", 4)
-                for tt in range(2):
-                    nc.vector.bn_aggr(out=mean_var[:, 2 * tt:2 * tt + 2], in_=bn_r[:, tt, :, :].rearrange("p j s -> p (j s)"))
-            if n + 1 < len(blocks):
-                centre_first(blocks[n + 1])
-            if n == 5:
+                r_mean_var = small("r_mean_var", 4)
+                for t in range(2):
+                    nc.vector.bn_aggr(out=r_mean_var[:, 2 * t:2 * t + 2], in_=bn_r[:, t, :, :].rearrange("p j s -> p (j s)"))
+            if n + 1 < BLOCKS:
+                centre_first(blocks[n + 1], neg_mean_r)
+            if n == stats_turn:
                 var = small("r_var", 2)
-                nc.vector.tensor_scalar(out=var[:], in0=mean_var[:, 1::2], scalar1=EPS, scalar2=None, op0=ALU.add)
-                late["rstd_second"] = inverse_root(var[:], "r_rstd")
+                nc.vector.tensor_scalar(out=var[:], in0=r_mean_var[:, 1::2], scalar1=EPS, scalar2=None, op0=ALU.add)
+                rstd_second = inverse_root(var[:], "r_rstd")
             gate_block(0, j, gate_banks())
-            if n < 5:
-                reads[0]()
-            if n + 1 < len(blocks):
-                scale_first(blocks[n + 1], "vector" if n < 4 else "scalar")
-            if n < 5:
-                reads[1]()
-            if n < 4:
-                scale_u(2 + n % 2, gate_cols((GATE_F, GATE_O)[n // 2]), "scalar")
-            if n == 4:
-                input_times_cell(0)
-            if n == 5:
-                input_times_cell(1)
-                late["offset"] = small("r_offset", 2)
-                nc.vector.scalar_tensor_tensor(out=late["offset"][:], in0=mean_var[:, 0::2], scalar=-1.0, in1=late["rstd_second"][:],
+            if n < first_round_turns:
+                reads[-2]()
+            if n + 1 < BLOCKS:
+                scale_first(blocks[n + 1], rstd_first, not late_scalings)
+            if n < first_round_turns:
+                reads[-1]()
+            if late_scalings:
+                scale_u(*late_scalings.pop(0), True)
+            if n in (stats_turn - 1, stats_turn):
+                input_times_cell(n - stats_turn + 1)
+            if n == stats_turn:
+                offset = small("r_offset", 2)
+                nc.vector.scalar_tensor_tensor(out=offset[:], in0=r_mean_var[:, 0::2], scalar=-1.0, in1=rstd_second[:],
                                                op0=ALU.mult, op1=ALU.mult)
-                second_round(blocks[0], False)
-            if n == 6:
+                second_round(blocks[0], rstd_second, offset)
+            if n == stats_turn + 1:
                 forget_times_c0(0, c0_banks[0])
-                second_round(blocks[1], False)
+                second_round(blocks[1], rstd_second, offset)
                 forget_times_c0(1, c0_banks[1])
-                cells[0] = back(0, (GATE_I, GATE_F), (7, 5))
-                gain_second(blocks[0], False)
-            if n == 7:
-                parts = cell_parts(cells[0])
-        for m, j in enumerate(blocks[:6]):
-            if m < 4:
-                second_round(blocks[m + 2], m + 2 in ())
-            if m < 5:
-                gain_second(blocks[m + 1], m + 1 in ())
+                cell = to_rows(0, (GATE_I, GATE_F), (7, 5))
+                gain_second(blocks[0])
+        parts = cell_parts(cell)
+
+        cell_blocks = blocks[:CELL_BLOCKS]
+        for n, j in enumerate(cell_blocks):
+            if n + 2 < len(cell_blocks):
+                second_round(cell_blocks[n + 2], rstd_second, offset)
+            if n + 1 < len(cell_blocks):
+                gain_second(cell_blocks[n + 1])
             gate_block(1, j, gate_banks())
-            if m == 0:
-                means[0] = cell_mean_var(parts)
-                rstds[0] = cell_rstd(means[0])
-                cell_centre(0, cells[0], means[0])
-                cells[1] = back(1, (GATE_I, GATE_F), (6, 7))
-            if m == 1:
-                cell_finish(0, rstds[0])
-                parts = cell_parts(cells[1])
-            if m == 2:
-                means[1] = cell_mean_var(parts)
-                rstds[1] = cell_rstd(means[1])
-                cell_centre(1, cells[1], means[1])
-            if m == 3:
+            if n in (0, 2):
+                mean_var = cell_mean_var(parts)
+                rstd = cell_rstd(mean_var)
+                cell_centre(n // 2, cell, mean_var)
+            if n == 0:
+                cell = to_rows(1, (GATE_I, GATE_F), (6, 7))
+            if n == 3:
                 c0_banks = [c0_transposed(t, 3 + t) for t in (2, 3)]
-                cell_finish(1, rstds[1])
-            if m == 4:
+            if n in (1, 3):
+                cell_finish(n // 2, rstd)
+            if n == 1:
+                parts = cell_parts(cell)
+            if n == 4:
                 input_times_cell(2)
                 input_times_cell(3)
-        second_round(blocks[6], False)
-        second_round(blocks[7], False, (7, 3))
+
+        o_first, o_second = blocks[CELL_BLOCKS:]
+        second_round(o_first, rstd_second, offset)
+        second_round(o_second, rstd_second, offset, (7, 3))
         forget_times_c0(2, c0_banks[0])
         forget_times_c0(3, c0_banks[1])
         cell_tanh(0)
-        cells[2] = back(2, (GATE_I, GATE_F), (4, 5))
-        gain_second(blocks[6], False)
-        cells[3] = back(3, (GATE_I, GATE_F), (6, 7))
-        parts = cell_parts(cells[2])
-        gate_block(1, blocks[6], (0, 1))
-        outs[0] = back(0, (GATE_O,), (3, 2))
-        gain_second(blocks[7], False)
-        means[2] = cell_mean_var(parts)
+        cell_2 = to_rows(2, (GATE_I, GATE_F), (4, 5))
+        gain_second(o_first)
+        cell_3 = to_rows(3, (GATE_I, GATE_F), (6, 7))
+        parts_2 = cell_parts(cell_2)
+        gate_block(1, o_first, (0, 1))
+        o_rows_0 = to_rows(0, (GATE_O,), (3, 2))
+        gain_second(o_second)
+        mean_var_2 = cell_mean_var(parts_2)
         cell_tanh(1)
-        parts = cell_parts(cells[3])
-        rstds[2] = cell_rstd(means[2])
-        gate_block(1, blocks[7], (0, 1))
-        cell_centre(2, cells[2], means[2])
-        means[3] = cell_mean_var(parts)
-        outs[1] = back(1, (GATE_O,), (4, 5))
-        hidden(0, outs[0])
-        rstds[3] = cell_rstd(means[3])
-        cell_centre(3, cells[3], means[3])
-        cell_finish(2, rstds[2])
+        parts_3 = cell_parts(cell_3)
+        rstd_2 = cell_rstd(mean_var_2)
+        gate_block(1, o_second, (0, 1))
+        cell_centre(2, cell_2, mean_var_2)
+        mean_var_3 = cell_mean_var(parts_3)
+        o_rows_1 = to_rows(1, (GATE_O,), (4, 5))
+        hidden(0, o_rows_0)
+        rstd_3 = cell_rstd(mean_var_3)
+        cell_centre(3, cell_3, mean_var_3)
+        cell_finish(2, rstd_2)
         cell_tanh(2)
-        cell_finish(3, rstds[3])
+        cell_finish(3, rstd_3)
         cell_tanh(3)
-        outs[2] = back(2, (GATE_O,), (3, 2))
-        outs[3] = back(3, (GATE_O,), (0, 1))
-        hidden(1, outs[1])
-        hidden(2, outs[2])
-        hidden(3, outs[3])
+        o_rows_2 = to_rows(2, (GATE_O,), (3, 2))
+        o_rows_3 = to_rows(3, (GATE_O,), (0, 1))
+        hidden(1, o_rows_1)
+        hidden(2, o_rows_2)
+        hidden(3, o_rows_3)

from contextlib import ExitStack

import concourse.mybir as mybir
from concourse.masks import make_identity

B, V, H = 512, 128, 1024
G = 4 * H
EPS = 1e-5
FLOPS = 2 * B * G * (H + V)

F32 = mybir.dt.float32
BF16 = mybir.dt.bfloat16
U32 = mybir.dt.uint32
U8 = mybir.dt.uint8
FP8X4 = mybir.dt.float8_e5m2_x4
ACT = mybir.ActivationFunctionType
ALU = mybir.AluOpType
AXIS = mybir.AxisListType

P = 128
TILES = B // P
BANK = 512
BLOCKS = G // BANK
CHUNKS = G // P
K_PASS = 4 * P
PASSES = H // K_PASS
GATE_I, GATE_F, GATE_G, GATE_O = 0, 1, 2, 3
STAGE_BUFS = 3
GROUPED_BUFS = 3
SMALL_BUFS = 3
STEPS = PASSES + BLOCKS * PASSES
A_STEPS = TILES * BLOCKS // 2
FIRST_R_STEP = PASSES + 3
A_RSTD_STEP = BLOCKS + 1
CELL_BLOCKS = 6


def tile_multilstm_pa_kernel(tc, x, h0, c0, w_ih1, w_hh1, lni_w1, lni_b1, lnh_w1, lnh_b1, lnc_w1, lnc_b1, out_0, out_1):
    nc = tc.nc
    with ExitStack() as ctx:
        keep = ctx.enter_context(tc.tile_pool(name="keep", bufs=1))
        shared = ctx.enter_context(tc.tile_pool(name="shared", bufs=1))
        psum = ctx.enter_context(tc.psum_pool(name="psum", bufs=1))
        ctx.enter_context(tc.manual_schedule())

        def bank(i, dtype=F32):
            width = BANK if dtype == F32 else 2 * BANK
            return psum.tile([P, width], dtype, name="bank%d" % i, tag="bank%d" % i)

        def stage_tile():
            return shared.tile([P, 4, H], BF16, name="stage", tag="stage", bufs=STAGE_BUFS, align_bytes=64, offset=0)

        def grouped_tile():
            return shared.tile([P, 4 * BANK], BF16, name="grouped", tag="grouped", bufs=GROUPED_BUFS, align_bytes=64,
                               offset=STAGE_BUFS * 4 * H * 2)

        def small(name, width):
            return keep.tile([P, width], F32, name=name, tag=name, bufs=SMALL_BUFS)

        def squares_tile():
            return keep.tile([P, BANK], BF16, name="squares", tag="squares", bufs=SMALL_BUFS)

        ident_f32 = keep.tile([P, P], F32, name="ident_f32")
        ident_bf16 = keep.tile([P, P], BF16, name="ident_bf16")
        neg_half = keep.tile([P, 2], F32, name="neg_half")
        vec_rows = keep.tile([P, P], BF16, name="vec_rows")
        bias_i = keep.tile([P, CHUNKS], F32, name="bias_i")
        bias = keep.tile([P, CHUNKS], F32, name="bias")
        x_rows = keep.tile([P, TILES, V], BF16, name="x_rows")
        x_t = keep.tile([P, B], BF16, name="x_t")
        x_t32 = keep.tile([P, B], F32, name="x_t32")
        wih_t = keep.tile([P, G], BF16, name="wih_t")
        wih_sums = keep.tile([P, 4], F32, name="wih_sums")
        neg_wih_mean = keep.tile([P, 1], F32, name="neg_wih_mean")
        neg_mean_a = keep.tile([P, TILES], F32, name="neg_mean_a")
        gain_i = keep.tile([P, G], BF16, name="gain_i")
        gain_h = keep.tile([P, G], BF16, name="gain_h")
        gain_c = keep.tile([P, H], BF16, name="gain_c")
        bias_c = keep.tile([P, H], BF16, name="bias_c")
        c_rows = keep.tile([P, TILES, H], BF16, name="c_rows")
        h_codes = keep.tile([P, PASSES, B], U32, name="h_codes", align_bytes=64)
        h_scales = keep.tile([P, PASSES, B], U8, name="h_scales", align_bytes=64)
        w_codes = keep.tile([P, BLOCKS, PASSES, BANK], U32, name="w_codes", align_bytes=64)
        w_scales = keep.tile([P, BLOCKS, PASSES, BANK], U8, name="w_scales", align_bytes=64)
        u = keep.tile([P, TILES, G], F32, name="u")
        v_pair = [keep.tile([P, 2, G], F32, name="v_first")]
        squares_a = keep.tile([P, TILES, BLOCKS], F32, name="squares_a")
        sums_r = keep.tile([P, 2, BLOCKS], F32, name="sums_r")
        squares_r = keep.tile([P, 2, BLOCKS], F32, name="squares_r")
        neg_shift = keep.tile([P, 2], F32, name="neg_shift")
        bn_r = keep.tile([P, 2, BLOCKS, 6], F32, name="bn_r")
        rstd_a = []

        def block_cols(j):
            return slice(j * BANK, (j + 1) * BANK)

        def gate_cols(gate):
            return slice(gate * H, (gate + 1) * H)

        def v_cols(t, cols):
            return v_pair[t // 2][:, t % 2, cols]

        def inverse_root(var, name):
            rstd = small(name, var.shape[1])
            nc.gpsimd.tensor_tensor(out=rstd[:], in0=var, in1=neg_half[:, :var.shape[1]], op=ALU.pow)
            return rstd

        def scale(ap, factor, on_scalar):
            if on_scalar:
                nc.scalar.activation(out=ap, in_=ap, func=ACT.Copy, scale=factor)
            else:
                nc.vector.tensor_scalar(out=ap, in0=ap, scalar1=factor, scalar2=None, op0=ALU.mult)

        def a_square(t, j, bk):
            squares = squares_tile()
            nc.scalar.activation(out=squares[:], in_=bk[:], func=ACT.Square, bias=neg_mean_a[:, t:t + 1],
                                 accum_out=squares_a[:, t, j:j + 1])

        def a_gain(t, j, bk):
            nc.vector.scalar_tensor_tensor(out=u[:, t, block_cols(j)], in0=bk[:], scalar=neg_mean_a[:, t:t + 1],
                                           in1=gain_i[:, block_cols(j)], op0=ALU.add, op1=ALU.mult)

        def a_sum(pair):
            total = small("a_total", 2)
            nc.vector.tensor_reduce(out=total[:], in_=squares_a[:, 2 * pair:2 * pair + 2, :], axis=AXIS.X, op=ALU.add)
            return total

        def a_rstd(total):
            var = small("a_var", 2)
            nc.vector.tensor_scalar(out=var[:], in0=total[:], scalar1=1.0 / G, scalar2=EPS, op0=ALU.mult, op1=ALU.add)
            rstd_a.append(inverse_root(var[:], "a_rstd"))

        def scale_u(t, gate, on_scalar):
            scale(u[:, t, gate_cols(gate)], rstd_a[t // 2][:, t % 2:t % 2 + 1], on_scalar)

        def r_matmul(t, j, i):
            bk = bank(i)
            rows = slice(t * P, (t + 1) * P)
            for q in range(PASSES):
                nc.tensor.matmul_mx(out=bk[:], lhsT=h_codes[:, q, rows].bitcast(FP8X4), lhsT_scale=h_scales[:, q, rows],
                                    rhs=w_codes[:, j, q, :].bitcast(FP8X4), rhs_scale=w_scales[:, j, q, :],
                                    start=(q == 0), stop=(q == PASSES - 1))
            return bk

        def r_copy(n, bk):
            j, t = divmod(n, 2)
            nc.scalar.activation(out=v_cols(t, block_cols(j)), in_=bk[:], func=ACT.Copy, accum_out=sums_r[:, t, j:j + 1])

        def r_square(n):
            j, t = divmod(n, 2)
            squares = squares_tile()
            nc.scalar.activation(out=squares[:], in_=v_cols(t, block_cols(j)), func=ACT.Square,
                                 bias=neg_shift[:, t:t + 1], accum_out=squares_r[:, t, j:j + 1])

        def first_round(n, i):
            j, t = divmod(n, 2)
            bk = r_matmul(2 + t, j, i)
            return lambda: nc.vector.bn_stats(out=bn_r[:, t, j, :], in_=bk[:])

        for k, vec in enumerate((lni_w1, lni_b1, lnh_b1)):
            nc.sync.dma_start(out=vec_rows[k * CHUNKS:(k + 1) * CHUNKS, :], in_=vec.rearrange("(c p) -> c p", p=P))
        nc.sync.dma_start(out=x_rows[:], in_=x.rearrange("(p t) v -> p t v", t=TILES))
        wih_stage = stage_tile()
        wih_rows = wih_stage[:].rearrange("p b (j c v) -> p (b j) c v", c=4, v=V)
        for gate in range(4):
            nc.sync.dma_start(out=wih_rows[:, 2 * gate:2 * (gate + 1), :, :],
                              in_=w_ih1[gate_cols(gate), :].rearrange("(j p c) v -> p j c v", p=P, c=4))
        h_stage = stage_tile()
        nc.sync.dma_start(out=h_stage[:], in_=h0.rearrange("(p t) k -> p t k", t=TILES))
        w_stage = []

        def load_w():
            rows = w_hh1[block_cols(len(w_stage)), :]
            w_stage.append(stage_tile())
            nc.sync.dma_start(out=w_stage[-1][:], in_=rows.rearrange("(b p) k -> p b k", p=P))

        load_w()
        nc.gpsimd.memset(vec_rows[3 * CHUNKS:, :], 0.0)
        make_identity(nc, ident_bf16[:])
        make_identity(nc, ident_f32[:])
        nc.gpsimd.memset(neg_half[:], -0.5)

        def spread_gain(gate, i):
            bk = bank(i, BF16)
            for c in range(H // P):
                row = gate * (H // P) + c
                nc.tensor.matmul(bk[:, c * P:(c + 1) * P], lhsT=ident_bf16[:, row:row + 1].to_broadcast([P, P]),
                                 rhs=vec_rows[:], start=True, stop=True)
            if gate == GATE_O:
                nc.vector.tensor_copy(out=gain_i[:, gate_cols(gate)], in_=bk[:])
            else:
                nc.scalar.copy(out=gain_i[:, gate_cols(gate)], in_=bk[:])

        def transpose_wih(gate, i):
            bk = bank(i, BF16)
            for jc in range(H // P):
                nc.tensor.transpose(bk[:, jc * P:(jc + 1) * P], wih_rows[:, 2 * gate + jc // 4, jc % 4, :], ident_bf16[:])
            dst = wih_t[:, gate_cols(gate)].rearrange("p (j r c) -> p j r c", j=2, c=4)
            src = bk[:].rearrange("p (j c r) -> p j r c", j=2, c=4)
            if gate % 2 == 0:
                nc.scalar.activation(out=dst, in_=src, func=ACT.Copy, accum_out=wih_sums[:, gate:gate + 1])
            else:
                nc.vector.tensor_scalar(out=dst, in0=src, scalar1=1.0, scalar2=None, op0=ALU.mult, op1=ALU.add,
                                        accum_out=wih_sums[:, gate:gate + 1])

        spread_gain(GATE_I, 5)
        spread_gain(GATE_F, 6)
        x_bank = bank(0, BF16)
        for t in range(TILES):
            nc.tensor.transpose(x_bank[:, t * P:(t + 1) * P], x_rows[:, t, :], ident_bf16[:])
        nc.vector.tensor_copy(out=x_t[:], in_=x_bank[:, :B])
        nc.vector.tensor_copy(out=x_t32[:], in_=x_bank[:, :B])
        for gate in range(4):
            transpose_wih(gate, 1 + gate)
        scaled_sums = small("scaled_sums", 4)
        nc.vector.tensor_scalar(out=scaled_sums[:], in0=wih_sums[:], scalar1=-1.0 / G, scalar2=None, op0=ALU.mult, op1=ALU.add,
                                accum_out=neg_wih_mean[:])
        load_w()
        spread_gain(GATE_G, 5)
        spread_gain(GATE_O, 6)

        def transpose_words(stage, q, s):
            banks = []
            for half in range(2):
                bk = bank((2 * s + half) % 3)
                view = bk[:].rearrange("p (b w r) -> p b w r", b=2, w=2)
                for b in range(2):
                    words = stage[:, 2 * half + b, :].bitcast(F32)
                    for w in range(2):
                        nc.tensor.transpose(view[:, b, w, :], words[:, q * K_PASS // 2 + w:(q + 1) * K_PASS // 2:2], ident_f32[:])
                banks.append(bk)
            return banks

        def interleave(grouped, half, bk, on_scalar):
            dst = grouped[:].bitcast(F32)[:, block_cols(half)].rearrange("p (b r w) -> p b r w", b=2, w=2)
            src = bk[:].rearrange("p (b w r) -> p b r w", b=2, w=2)
            if on_scalar:
                nc.scalar.copy(out=dst, in_=src)
            else:
                nc.vector.tensor_copy(out=dst, in_=src)

        grouped = []
        a_units = []
        reads = []
        early_scalings = [(t, gate) for gate in (GATE_I, GATE_F) for t in range(2)]
        for s in range(STEPS + 1):
            w_block, q = divmod(s - PASSES, PASSES)
            last_a_units = a_units
            a_units = []
            if 1 <= s <= A_STEPS:
                for k in range(2):
                    t, j = divmod(2 * (s - 1) + k, BLOCKS)
                    bk = bank(4 + 2 * (s % 2) + k)
                    nc.tensor.matmul(bk[:], lhsT=x_t[:, t * P:(t + 1) * P], rhs=wih_t[:, block_cols(j)], start=True, stop=True)
                    a_units.append((t, j, bk))
            if s > A_STEPS:
                for k in range(2):
                    reads.append(first_round(len(reads), 4 + 2 * (s % 2) + k))
            if s < STEPS:
                word_banks = transpose_words(h_stage if w_block < 0 else w_stage[w_block], q, s)
                grouped.append(grouped_tile())
                if q == PASSES - 1 and len(w_stage) < BLOCKS:
                    load_w()
                if q == PASSES - 1 and w_block + STAGE_BUFS == BLOCKS:
                    nc.sync.dma_start(out=gain_h[:], in_=lnh_w1.partition_broadcast(P))
                    nc.sync.dma_start(out=c_rows[:], in_=c0.rearrange("(p t) h -> p t h", t=TILES))
                    nc.sync.dma_start(out=gain_c[:], in_=lnc_w1.partition_broadcast(P))
                    nc.sync.dma_start(out=bias_c[:], in_=lnc_b1.partition_broadcast(P))
            if s == 0:
                mean_bank = bank(3)
                for t in range(TILES):
                    nc.tensor.matmul(mean_bank[:, t:t + 1], lhsT=x_t32[:, t * P:(t + 1) * P], rhs=neg_wih_mean[:], start=True, stop=True)
                nc.vector.tensor_copy(out=neg_mean_a[:], in_=mean_bank[:, :TILES])
            if s == FIRST_R_STEP - 3:
                bias_bank = bank(3, BF16)
                nc.tensor.transpose(bias_bank[:, :P], vec_rows[:], ident_bf16[:])
            unit = s - FIRST_R_STEP
            if unit >= 1:
                r_copy(unit - 1, r_bank)
            for a_unit in last_a_units:
                a_gain(*a_unit)
            for a_unit in a_units:
                a_square(*a_unit)
            if unit in (1, 2):
                nc.scalar.activation(out=neg_shift[:, unit - 1:unit], in_=sums_r[:, unit - 1, 0:1], func=ACT.Copy, scale=-1.0 / BANK)
            if s in (A_RSTD_STEP, STEPS):
                a_total = a_sum(len(rstd_a))
            if s == STEPS:
                reads[0]()
            if s >= 1:
                last_block, last_q = divmod(s - 1 - PASSES, PASSES)
                codes = h_codes[:, last_q, :] if last_block < 0 else w_codes[:, last_block, last_q, :]
                scales = h_scales[:, last_q, :] if last_block < 0 else w_scales[:, last_block, last_q, :]
                nc.vector.quantize_mx(out=codes.bitcast(FP8X4), scales=scales, in_=grouped[s - 1][:])
            if s in (A_RSTD_STEP, STEPS):
                a_rstd(a_total)
            if unit >= 0:
                r_bank = r_matmul(unit % 2, unit // 2, 3)
            if unit >= 2:
                r_square(unit - 2)
            if s == STEPS:
                r_square(unit - 1)
            scales_u = s > A_RSTD_STEP and len(early_scalings) > 0
            if scales_u:
                scale_u(*early_scalings.pop(0), False)
            if s == FIRST_R_STEP - 2:
                nc.scalar.copy(out=bias_i[:], in_=bias_bank[:, CHUNKS:2 * CHUNKS])
            if s == FIRST_R_STEP - 1:
                nc.vector.tensor_tensor(out=bias[:], in0=bias_bank[:, 2 * CHUNKS:3 * CHUNKS], in1=bias_i[:], op=ALU.add)
            if s < STEPS:
                scalar_takes_both = s in range(2, FIRST_R_STEP, 2)
                vector_takes_both = FIRST_R_STEP <= s <= A_STEPS and not scales_u and s % 3 != 1
                interleave(grouped[s], 0, word_banks[0], scalar_takes_both)
                interleave(grouped[s], 1, word_banks[1], not vector_takes_both)

        v_pair.append(shared.tile([P, 2, G], F32, name="v_second", tag="v_second", align_bytes=64, offset=0))

        def centre_first(j, neg_mean):
            for t in range(2):
                ap = v_cols(t, block_cols(j))
                nc.vector.scalar_tensor_tensor(out=ap, in0=ap, scalar=neg_mean[:, t:t + 1], in1=gain_h[:, block_cols(j)],
                                               op0=ALU.add, op1=ALU.mult)

        def scale_first(j, rstd, on_scalar):
            for t in range(2):
                scale(v_cols(t, block_cols(j)), rstd[:, t:t + 1], on_scalar)

        def second_round(j, rstd, offset, banks=(3, 4)):
            tiles = [r_matmul(2 + t, j, banks[t]) for t in range(2)]
            for t in range(2):
                nc.scalar.activation(out=v_cols(2 + t, block_cols(j)), in_=tiles[t][:], func=ACT.Identity,
                                     scale=rstd[:, t:t + 1], bias=offset[:, t:t + 1])

        def gain_second(j):
            both = v_pair[1][:, :, block_cols(j)]
            nc.vector.tensor_tensor(out=both, in0=both, in1=gain_h[:, block_cols(j)].unsqueeze(1).to_broadcast([P, 2, BANK]),
                                    op=ALU.mult)

        def transpose_sum(out, terms):
            for k, term in enumerate(terms):
                nc.tensor.matmul(out, lhsT=term, rhs=ident_f32[:], start=(k == 0), stop=(k == len(terms) - 1), is_transpose=True)

        def gate_block(pair, j, banks):
            for half in range(2):
                bk = bank(banks[half])
                view = bk[:].rearrange("p (c t b) -> p c t b", c=2, t=2)
                chunks = [4 * j + 2 * half + c for c in range(2)]
                for c, chunk in enumerate(chunks):
                    cols = slice(chunk * P, (chunk + 1) * P)
                    for t in range(2):
                        transpose_sum(view[:, c, t, :], [u[:, 2 * pair + t, cols], v_cols(2 * pair + t, cols)])
                for c, chunk in enumerate(chunks):
                    nc.scalar.activation(out=v_pair[pair][:, :, chunk * P:(chunk + 1) * P], in_=view[:, c, :, :],
                                         func=ACT.Tanh if j // 2 == GATE_G else ACT.Sigmoid, bias=bias[:, chunk:chunk + 1])

        def input_times_cell(t):
            ap = v_cols(t, gate_cols(GATE_I))
            nc.vector.tensor_tensor(out=ap, in0=ap, in1=v_cols(t, gate_cols(GATE_G)), op=ALU.mult)

        def c0_transposed(t, i):
            bk = bank(i, BF16)
            for j in range(H // P):
                nc.tensor.transpose(bk[:, j * P:(j + 1) * P], c_rows[:, t, j * P:(j + 1) * P], ident_bf16[:])
            return bk

        def forget_times_c0(t, bk):
            ap = v_cols(t, gate_cols(GATE_F))
            nc.vector.tensor_tensor(out=ap, in0=bk[:], in1=ap, op=ALU.mult)

        def to_rows(t, gates, banks):
            tiles = []
            for half in range(2):
                bk = bank(banks[half])
                for c in range(BANK // P):
                    first = half * BANK + c * P
                    transpose_sum(bk[:, c * P:(c + 1) * P], [v_cols(t, slice(gate * H + first, gate * H + first + P)) for gate in gates])
                tiles.append(bk)
            return tiles

        def cell_parts(tiles):
            parts = small("c_parts", 12)
            for half in range(2):
                nc.vector.bn_stats(out=parts[:, 6 * half:6 * half + 6], in_=tiles[half][:])
            return parts

        def cell_mean_var(parts):
            mean_var = small("c_mean_var", 2)
            nc.vector.bn_aggr(out=mean_var[:], in_=parts[:])
            return mean_var

        def cell_rstd(mean_var):
            var = small("c_var", 1)
            nc.vector.tensor_scalar(out=var[:], in0=mean_var[:, 1:2], scalar1=EPS, scalar2=None, op0=ALU.add)
            return inverse_root(var[:], "c_rstd")

        def cell_centre(t, tiles, mean_var):
            for half in range(2):
                nc.vector.scalar_tensor_tensor(out=u[:, t, block_cols(half)], in0=tiles[half][:], scalar=mean_var[:, 0:1],
                                               in1=gain_c[:, block_cols(half)], op0=ALU.subtract, op1=ALU.mult)

        def cell_finish(t, rstd):
            cy = u[:, t, 0:H]
            nc.vector.scalar_tensor_tensor(out=cy, in0=cy, scalar=rstd[:], in1=bias_c[:], op0=ALU.mult, op1=ALU.add)
            nc.sync.dma_start(out=out_1.rearrange("(p t) h -> p t h", t=TILES)[:, t, :], in_=cy)

        def cell_tanh(t):
            nc.scalar.activation(out=u[:, t, H:2 * H], in_=u[:, t, 0:H], func=ACT.Tanh)

        def hidden(t, tiles):
            for half in range(2):
                ap = u[:, t, H + half * BANK:H + (half + 1) * BANK]
                nc.vector.tensor_tensor(out=ap, in0=tiles[half][:], in1=ap, op=ALU.mult)
            nc.sync.dma_start(out=out_0.rearrange("(p t) h -> p t h", t=TILES)[:, t, :], in_=u[:, t, H:2 * H])

        last_units = [2 * BLOCKS - 2, 2 * BLOCKS - 1]
        last_banks = [r_matmul(n % 2, n // 2, n % 2) for n in last_units]
        r_copy(unit, r_bank)
        reads.extend([first_round(4, 2), first_round(5, 3)])
        for n, bk in zip(last_units, last_banks):
            r_copy(n, bk)
        for n in [unit] + last_units:
            r_square(n)
        reads[1]()
        reads[2]()
        for t in range(2):
            scale_u(t, GATE_G, False)
        total = small("r_total", 2)
        nc.vector.tensor_reduce(out=total[:], in_=sums_r[:], axis=AXIS.X, op=ALU.add)
        scale_u(0, GATE_O, False)
        neg_mean_r = small("r_neg_mean", 2)
        nc.vector.tensor_scalar(out=neg_mean_r[:], in0=total[:], scalar1=-1.0 / G, scalar2=None, op0=ALU.mult)
        terms = small("r_terms", 6)
        nc.vector.scalar_tensor_tensor(out=terms[:, 0:2], in0=total[:], scalar=1.0 / G, in1=neg_shift[:], op0=ALU.mult, op1=ALU.add)
        nc.vector.scalar_tensor_tensor(out=terms[:, 2:4], in0=total[:], scalar=-1.0 / G, in1=neg_shift[:], op0=ALU.mult,
                                       op1=ALU.subtract)
        scale_u(1, GATE_O, False)
        blocks = [2 * gate + half for gate in (GATE_I, GATE_G, GATE_F, GATE_O) for half in range(2)]
        centre_first(blocks[0], neg_mean_r)
        total = small("r_total", 2)
        nc.vector.tensor_reduce(out=total[:], in_=squares_r[:], axis=AXIS.X, op=ALU.add)
        reads[3]()
        nc.vector.tensor_scalar(out=terms[:, 4:6], in0=total[:], scalar1=1.0 / G, scalar2=EPS, op0=ALU.mult, op1=ALU.add)
        var = small("r_var", 2)
        for t in range(2):
            nc.vector.scalar_tensor_tensor(out=var[:, t:t + 1], in0=terms[:, t:t + 1], scalar=terms[:, 2 + t:3 + t],
                                           in1=terms[:, 4 + t:5 + t], op0=ALU.mult, op1=ALU.add)
        rstd_first = inverse_root(var[:], "r_rstd")
        for gate in (GATE_I, GATE_G):
            for t in (2, 3):
                scale_u(t, gate, True)
        reads[4]()
        reads[5]()
        scale_first(blocks[0], rstd_first, False)

        turns = [0]

        def gate_banks():
            turns[0] += 1
            return (2 * turns[0] % 3, (2 * turns[0] + 1) % 3)

        first_round_turns = (2 * BLOCKS - len(reads)) // 2
        stats_turn = first_round_turns
        late_scalings = [(t, gate) for gate in (GATE_F, GATE_O) for t in (2, 3)]
        for n, j in enumerate(blocks):
            if n < first_round_turns:
                reads.extend([first_round(len(reads) + k, 4 + (2 * n + k) % 4) for k in range(2)])
            if n == stats_turn:
                c0_banks = [c0_transposed(t, 5 + t) for t in range(2)]
                r_mean_var = small("r_mean_var", 4)
                for t in range(2):
                    nc.vector.bn_aggr(out=r_mean_var[:, 2 * t:2 * t + 2], in_=bn_r[:, t, :, :].rearrange("p j s -> p (j s)"))
            if n + 1 < BLOCKS:
                centre_first(blocks[n + 1], neg_mean_r)
            if n == stats_turn:
                var = small("r_var", 2)
                nc.vector.tensor_scalar(out=var[:], in0=r_mean_var[:, 1::2], scalar1=EPS, scalar2=None, op0=ALU.add)
                rstd_second = inverse_root(var[:], "r_rstd")
            gate_block(0, j, gate_banks())
            if n < first_round_turns:
                reads[-2]()
            if n + 1 < BLOCKS:
                scale_first(blocks[n + 1], rstd_first, not late_scalings)
            if n < first_round_turns:
                reads[-1]()
            if late_scalings:
                scale_u(*late_scalings.pop(0), True)
            if n in (stats_turn - 1, stats_turn):
                input_times_cell(n - stats_turn + 1)
            if n == stats_turn:
                offset = small("r_offset", 2)
                nc.vector.scalar_tensor_tensor(out=offset[:], in0=r_mean_var[:, 0::2], scalar=-1.0, in1=rstd_second[:],
                                               op0=ALU.mult, op1=ALU.mult)
                second_round(blocks[0], rstd_second, offset)
            if n == stats_turn + 1:
                forget_times_c0(0, c0_banks[0])
                second_round(blocks[1], rstd_second, offset)
                forget_times_c0(1, c0_banks[1])
                cell = to_rows(0, (GATE_I, GATE_F), (7, 5))
                gain_second(blocks[0])
        parts = cell_parts(cell)

        cell_blocks = blocks[:CELL_BLOCKS]
        for n, j in enumerate(cell_blocks):
            if n + 2 < len(cell_blocks):
                second_round(cell_blocks[n + 2], rstd_second, offset)
            if n + 1 < len(cell_blocks):
                gain_second(cell_blocks[n + 1])
            gate_block(1, j, gate_banks())
            if n in (0, 2):
                mean_var = cell_mean_var(parts)
                rstd = cell_rstd(mean_var)
                cell_centre(n // 2, cell, mean_var)
            if n == 0:
                cell = to_rows(1, (GATE_I, GATE_F), (6, 7))
            if n == 3:
                c0_banks = [c0_transposed(t, 3 + t) for t in (2, 3)]
            if n in (1, 3):
                cell_finish(n // 2, rstd)
            if n == 1:
                parts = cell_parts(cell)
            if n == 4:
                input_times_cell(2)
                input_times_cell(3)

        o_first, o_second = blocks[CELL_BLOCKS:]
        second_round(o_first, rstd_second, offset)
        second_round(o_second, rstd_second, offset, (7, 3))
        forget_times_c0(2, c0_banks[0])
        forget_times_c0(3, c0_banks[1])
        cell_tanh(0)
        cell_2 = to_rows(2, (GATE_I, GATE_F), (4, 5))
        gain_second(o_first)
        cell_3 = to_rows(3, (GATE_I, GATE_F), (6, 7))
        parts_2 = cell_parts(cell_2)
        gate_block(1, o_first, (0, 1))
        o_rows_0 = to_rows(0, (GATE_O,), (3, 2))
        gain_second(o_second)
        mean_var_2 = cell_mean_var(parts_2)
        cell_tanh(1)
        parts_3 = cell_parts(cell_3)
        rstd_2 = cell_rstd(mean_var_2)
        gate_block(1, o_second, (0, 1))
        cell_centre(2, cell_2, mean_var_2)
        mean_var_3 = cell_mean_var(parts_3)
        o_rows_1 = to_rows(1, (GATE_O,), (4, 5))
        hidden(0, o_rows_0)
        rstd_3 = cell_rstd(mean_var_3)
        cell_centre(3, cell_3, mean_var_3)
        cell_finish(2, rstd_2)
        cell_tanh(2)
        cell_finish(3, rstd_3)
        cell_tanh(3)
        o_rows_2 = to_rows(2, (GATE_O,), (3, 2))
        o_rows_3 = to_rows(3, (GATE_O,), (0, 1))
        hidden(1, o_rows_1)
        hidden(2, o_rows_2)
        hidden(3, o_rows_3)
